import numpy as np
import ml_dtypes


def mxq(x, axis, fmt="e4m3"):
    dtype, down = {"e4m3": (ml_dtypes.float8_e4m3fn, 7), "e5m2": (ml_dtypes.float8_e5m2, 14)}[fmt]
    v = np.moveaxis(np.asarray(x, np.float32).astype(ml_dtypes.bfloat16).astype(np.float64), axis, -1)
    blocks = v.reshape(v.shape[:-1] + (-1, 32))
    amax = np.abs(blocks).max(-1, keepdims=True)
    byte = np.maximum(np.where(amax > 0, np.frexp(amax)[1] - 1 + 127, 0) - down, 1)
    scale = np.exp2(byte - 127.0)
    codes = (blocks / scale).astype(np.float32).astype(dtype).astype(np.float64)
    return np.moveaxis((codes * scale).reshape(v.shape), -1, axis)


WIDE = False


def mx_kscale(k):
    if not WIDE:
        return np.ones(k)
    levels = np.array([10, -10, 5, -5, 0])
    a = np.random.permutation(np.resize(levels, k // 512 * 4)).reshape(k // 512, 4)
    idx = np.arange(k)
    return np.exp2(a[idx // 512, idx % 128 // 32])


BF16 = ml_dtypes.bfloat16


def bf(x):
    return np.asarray(x, np.float32).astype(BF16)


def f64(x):
    return np.asarray(x).astype(np.float64)


B, C, H, W = 2, 1024, 32, 32
N = H * W
KV = 0.05 * N / np.sqrt(C)


def setup_inputs():
    s, t = mx_kscale(C), mx_kscale(C)
    return {"x": bf(np.random.standard_normal((B, C, H, W)) * s[None, :, None, None]),
            "mask": bf(np.random.random_sample((B, 1, H, W))),
            "W_q": bf(np.random.standard_normal((C, C)) / np.sqrt(C) / s[:, None]),
            "b_q": bf(np.random.standard_normal(C) * 0.3),
            "kv_know": bf(np.random.standard_normal((B, 1, C)) * KV * t),
            "kv_mask": bf(np.random.standard_normal((B, 1, C)) * KV * t),
            "W_out": bf(np.random.standard_normal((C, C)) / KV / t[:, None]),
            "b_out": bf(np.random.standard_normal(C) * 0.2)}


def reference(x, mask, W_q, b_q, kv_know, kv_mask, W_out, b_out):
    x, mask = f64(x), f64(mask)
    b, c, h, w = x.shape
    xf = np.transpose(x, (0, 2, 3, 1)).reshape(b, h * w, c)
    q = (mxq(xf, 2, "e4m3") @ mxq(f64(W_q), 0, "e4m3")) + f64(b_q)
    q = q / np.linalg.norm(q, axis=-1, keepdims=True)
    m = np.transpose(mask, (0, 2, 3, 1)).reshape(b, h * w, 1)
    inv = 1.0 - m
    qu = q * inv
    qm = q * m
    out_know = f64(kv_know) * qu
    out_mask = f64(kv_mask) * qm
    out = out_know * inv + m * (0.3 * out_know + 0.7 * out_mask)
    return (mxq(out, 2, "e4m3") @ mxq(f64(W_out), 0, "e4m3")) + f64(b_out)

@@ -1,0 +1,324 @@
+from contextlib import ExitStack
+
+import concourse.mybir as mybir
+from concourse.masks import make_identity
+
+F32 = mybir.dt.float32
+BF16 = mybir.dt.bfloat16
+U32 = mybir.dt.uint32
+U8 = mybir.dt.uint8
+FP8X4 = mybir.dt.float8_e4m3fn_x4
+ACT = mybir.ActivationFunctionType
+ALU = mybir.AluOpType
+AXIS = mybir.AxisListType
+
+P = 128
+PACK = 4
+K_PASS = P * PACK
+IMAGES = 2
+CHANNELS = 1024
+PIXELS = 1024
+PASSES = CHANNELS // K_PASS
+C_TILES = CHANNELS // P
+CHUNK = 512
+CHUNKS = IMAGES * PIXELS // CHUNK
+BLOCKS = CHUNK // P
+HALF = CHANNELS // 2
+STEPS = 8
+TERMS = 3
+
+FLOPS = 2 * 2 * IMAGES * PIXELS * CHANNELS * CHANNELS
+
+
+def tile_hydraattention_pb_kernel(tc, x, mask, W_q, b_q, kv_know, kv_mask, W_out, b_out, out):
+    nc = tc.nc
+    x_rows = x.rearrange("b c h w -> b c (h w)")
+
+    with ExitStack() as ctx:
+        keep = ctx.enter_context(tc.tile_pool(name="keep", bufs=1))
+        raw_pool = ctx.enter_context(tc.tile_pool(name="raw", bufs=12))
+        grouped_pool = ctx.enter_context(tc.tile_pool(name="grouped", bufs=3))
+        u_pool = ctx.enter_context(tc.tile_pool(name="u", bufs=3))
+        small = ctx.enter_context(tc.tile_pool(name="small", bufs=2))
+        junk_pool = ctx.enter_context(tc.tile_pool(name="junk", bufs=4))
+        gated_pool = ctx.enter_context(tc.tile_pool(name="gated", bufs=3))
+        y_pool = ctx.enter_context(tc.tile_pool(name="y", bufs=8))
+        psum = ctx.enter_context(tc.psum_pool(name="psum", bufs=4))
+        ctx.enter_context(tc.manual_schedule())
+
+        wq_codes = keep.tile([P, PASSES, CHANNELS], U32, align_bytes=64)
+        wq_scales = keep.tile([P, PASSES, CHANNELS], U8, align_bytes=64)
+        wo_codes = keep.tile([P, PASSES, CHANNELS], U32, align_bytes=64)
+        wo_scales = keep.tile([P, PASSES, CHANNELS], U8, align_bytes=64)
+        x_codes = keep.tile([P, CHUNKS, PASSES, CHUNK], U32, align_bytes=64)
+        x_scales = keep.tile([P, CHUNKS, PASSES, CHUNK], U8, align_bytes=64)
+        g_codes = keep.tile([P, CHUNKS * BLOCKS, PASSES, P], U32, align_bytes=64)
+        g_scales = keep.tile([P, CHUNKS * BLOCKS, PASSES, P], U8, align_bytes=64)
+        ident_f32 = keep.tile([P, P], F32)
+        ident_bf16 = keep.tile([P, P], BF16)
+        vectors = keep.tile([P, P], BF16)
+        columns = keep.tile([P, CHUNKS * BLOCKS + C_TILES], F32)
+        mix = keep.tile([P, CHUNKS * BLOCKS, 2], F32)
+        kv_rows = keep.tile([P, IMAGES, CHANNELS], BF16)
+        bout_bc = keep.tile([P, CHANNELS], BF16)
+        split_a = keep.tile([P, BLOCKS, P], BF16)
+        split_b = keep.tile([P, BLOCKS, P], BF16)
+        splits = [split_a, split_b]
+        minus_half = keep.tile([P, BLOCKS], F32)
+
+        def x_unit(k, g):
+            cols = slice((k % 2) * CHUNK, (k % 2 + 1) * CHUNK)
+            return x_rows[k // 2, g * K_PASS : (g + 1) * K_PASS, cols].rearrange("(p j) t -> p j t", j=PACK)
+
+        def wq_unit(g, h):
+            return W_q[g * K_PASS : (g + 1) * K_PASS, h * HALF : (h + 1) * HALF].rearrange("(p j) n -> p j n", j=PACK)
+
+        def wo_unit(g, h):
+            return W_out[g * K_PASS : (g + 1) * K_PASS, h * HALF : (h + 1) * HALF].rearrange("(j p) n -> p j n", p=P)
+
+        def load(source, label):
+            raw = raw_pool.tile([P, PACK, CHUNK], BF16, name=label, tag="raw")
+            nc.sync.dma_start(out=raw[:], in_=source)
+            return raw
+
+        nc.vector.memset(vectors[:], 0.0)
+        nc.vector.memset(kv_rows[:], 0.0)
+        nc.vector.memset(minus_half[:], -0.5)
+        nc.vector.memset(split_a[:], 0.0)
+        nc.vector.memset(split_b[:], 0.0)
+        make_identity(nc, ident_bf16[:])
+        make_identity(nc, ident_f32[:])
+
+        nc.sync.dma_start(
+            out=vectors[0 : CHUNKS * BLOCKS, :], in_=mask.rearrange("b o (r a) w -> (b o r) (a w)", a=4)
+        )
+        nc.sync.dma_start(
+            out=vectors[CHUNKS * BLOCKS : CHUNKS * BLOCKS + C_TILES, :], in_=b_q.rearrange("(r c) -> r c", c=P)
+        )
+        x_raw = {}
+        wq_raw = {}
+        wo_raw = {}
+        x_raw[0, 0] = load(x_unit(0, 0), "x_raw00")
+        wq_raw[0, 0] = load(wq_unit(0, 0), "wq_raw00")
+        x_raw[0, 1] = load(x_unit(0, 1), "x_raw01")
+        wq_raw[1, 0] = load(wq_unit(1, 0), "wq_raw10")
+        wq_raw[0, 1] = load(wq_unit(0, 1), "wq_raw01")
+        wq_raw[1, 1] = load(wq_unit(1, 1), "wq_raw11")
+        for g in range(PASSES):
+            x_raw[1, g] = load(x_unit(1, g), "x_raw1%d" % g)
+        for h in range(2):
+            for g in range(PASSES):
+                wo_raw[g, h] = load(wo_unit(g, h), "wo_raw%d%d" % (g, h))
+        for k in range(2, CHUNKS):
+            for g in range(PASSES):
+                x_raw[k, g] = load(x_unit(k, g), "x_raw%d%d" % (k, g))
+
+        nc.scalar.dma_start(
+            out=kv_rows[0:TERMS].rearrange("r b c -> r (b c)"),
+            in_=kv_know.rearrange("b o c -> (b o c)").partition_broadcast(TERMS),
+        )
+        nc.scalar.dma_start(
+            out=kv_rows[TERMS : 2 * TERMS].rearrange("r b c -> r (b c)"),
+            in_=kv_mask.rearrange("b o c -> (b o c)").partition_broadcast(TERMS),
+        )
+        nc.scalar.dma_start(out=bout_bc[:], in_=b_out.partition_broadcast(P))
+
+        def regroup(raw_cols, width, vector_cols):
+            grouped = grouped_pool.tile([P, width, PACK], BF16, tag="grouped", align_bytes=64)
+            if vector_cols > 0:
+                nc.vector.tensor_copy(
+                    out=grouped[:, 0:vector_cols, :].rearrange("p (c i) j -> p c j i", i=4),
+                    in_=raw_cols[:, :, 0:vector_cols].rearrange("p j (c i) -> p c j i", i=4),
+                )
+            if vector_cols < width:
+                nc.scalar.copy(
+                    out=grouped[:, vector_cols:width, :].rearrange("p (c i) j -> p c j i", i=4),
+                    in_=raw_cols[:, :, vector_cols:width].rearrange("p j (c i) -> p c j i", i=4),
+                )
+            return grouped
+
+        def quantise(grouped, codes, scales):
+            nc.vector.quantize_mx(
+                out=codes.bitcast(FP8X4), scales=scales, in_=grouped[:].rearrange("p w j -> p (w j)")
+            )
+
+        vec_ps = psum.tile([P, P], BF16, tag="to_scalar")
+        nc.tensor.transpose(vec_ps[:], vectors[:], ident_bf16[:])
+        nc.vector.tensor_copy(out=columns[:], in_=vec_ps[:, 0 : CHUNKS * BLOCKS + C_TILES])
+        m_col = columns[:, 0 : CHUNKS * BLOCKS]
+        bq_col = columns[:, CHUNKS * BLOCKS : CHUNKS * BLOCKS + C_TILES]
+        inv = keep.tile([P, CHUNKS * BLOCKS], F32)
+        blend = keep.tile([P, CHUNKS * BLOCKS], F32)
+        nc.vector.tensor_scalar(out=inv[:], in0=m_col, scalar1=-1.0, scalar2=1.0, op0=ALU.mult, op1=ALU.add)
+        nc.vector.scalar_tensor_tensor(out=blend[:], in0=m_col, scalar=0.3, in1=inv[:], op0=ALU.mult, op1=ALU.add)
+        nc.vector.tensor_tensor(out=mix[:, :, 0], in0=blend[:], in1=inv[:], op=ALU.mult)
+        nc.vector.scalar_tensor_tensor(out=mix[:, :, 1], in0=m_col, scalar=0.7, in1=m_col, op0=ALU.mult, op1=ALU.mult)
+
+        head = [
+            (x_raw[0, 0], x_codes[:, 0, 0, :], x_scales[:, 0, 0, :]),
+            (wq_raw[0, 0], wq_codes[:, 0, 0:HALF], wq_scales[:, 0, 0:HALF]),
+            (x_raw[0, 1], x_codes[:, 0, 1, :], x_scales[:, 0, 1, :]),
+            (wq_raw[1, 0], wq_codes[:, 1, 0:HALF], wq_scales[:, 1, 0:HALF]),
+            (wq_raw[0, 1], wq_codes[:, 0, HALF:CHANNELS], wq_scales[:, 0, HALF:CHANNELS]),
+            (wq_raw[1, 1], wq_codes[:, 1, HALF:CHANNELS], wq_scales[:, 1, HALF:CHANNELS]),
+        ]
+        waiting = None
+        for raw, codes, scales in head:
+            grouped = regroup(raw[:], CHUNK, CHUNK // 2)
+            if waiting is not None:
+                quantise(*waiting)
+            waiting = (grouped, codes, scales)
+        quantise(*waiting)
+
+        u_tiles = {}
+        sumsq_parts = {}
+        gate_rows = {}
+        gated = {}
+
+        def stage1_tile(k, ct):
+            if ct == 0:
+                u_tiles[k] = u_pool.tile([P, C_TILES, CHUNK], F32, name="u%d" % k, tag="u")
+            q_ps = psum.tile([P, CHUNK], F32, tag="to_scalar")
+            cols = slice(ct * P, (ct + 1) * P)
+            for g in range(PASSES):
+                nc.tensor.matmul_mx(
+                    out=q_ps[:],
+                    lhsT=wq_codes[:, g, cols].bitcast(FP8X4),
+                    lhsT_scale=wq_scales[:, g, cols],
+                    rhs=x_codes[:, k, g, :].bitcast(FP8X4),
+                    rhs_scale=x_scales[:, k, g, :],
+                    start=(g == 0),
+                    stop=(g == PASSES - 1),
+                )
+            nc.scalar.activation(
+                out=u_tiles[k][:, ct, :], in_=q_ps[:], func=ACT.Identity, bias=bq_col[:, ct : ct + 1], scale=1.0
+            )
+
+        def norm_group(k, i):
+            half, tb = i // BLOCKS, i % BLOCKS
+            if i == 0:
+                sumsq_parts[k] = small.tile([P, BLOCKS, 2], F32, name="parts%d" % k, tag="parts")
+            ut_ps = psum.tile([P, PACK, P], F32, tag="to_scalar")
+            for j in range(PACK):
+                nc.tensor.transpose(
+                    ut_ps[:, j, :], u_tiles[k][:, half * PACK + j, tb * P : (tb + 1) * P], ident_f32[:]
+                )
+            junk = junk_pool.tile([P, PACK * P], BF16, tag="junk")
+            nc.scalar.activation(
+                out=junk[:],
+                in_=ut_ps[:].rearrange("p j c -> p (j c)"),
+                func=ACT.Square,
+                accum_out=sumsq_parts[k][:, tb, half : half + 1],
+            )
+
+        def gate_scalars(k):
+            sumsq = small.tile([P, BLOCKS], F32, tag="sumsq")
+            rnorm = small.tile([P, BLOCKS], F32, tag="rnorm")
+            weights = small.tile([P, BLOCKS, 2], F32, tag="weights")
+            rest1 = small.tile([P, BLOCKS, 2], F32, tag="rest1")
+            rest2 = small.tile([P, BLOCKS, 2], F32, tag="rest2")
+            split = splits[k % 2]
+            nc.gpsimd.tensor_tensor(out=sumsq[:], in0=sumsq_parts[k][:, :, 0], in1=sumsq_parts[k][:, :, 1], op=ALU.add)
+            nc.gpsimd.tensor_tensor(out=rnorm[:], in0=sumsq[:], in1=minus_half[:], op=ALU.pow)
+            nc.gpsimd.tensor_tensor(
+                out=weights[:],
+                in0=mix[:, k * BLOCKS : (k + 1) * BLOCKS, :],
+                in1=rnorm[:].unsqueeze(2).to_broadcast([P, BLOCKS, 2]),
+                op=ALU.mult,
+            )
+            nc.gpsimd.tensor_copy(out=split[:, :, 0 : 2 * TERMS : TERMS], in_=weights[:])
+            nc.gpsimd.tensor_tensor(out=rest1[:], in0=weights[:], in1=split[:, :, 0 : 2 * TERMS : TERMS], op=ALU.subtract)
+            nc.gpsimd.tensor_copy(out=split[:, :, 1 : 2 * TERMS : TERMS], in_=rest1[:])
+            nc.gpsimd.tensor_tensor(out=rest2[:], in0=rest1[:], in1=split[:, :, 1 : 2 * TERMS : TERMS], op=ALU.subtract)
+            nc.gpsimd.tensor_copy(out=split[:, :, 2 : 2 * TERMS : TERMS], in_=rest2[:])
+
+        def gate_transposes(k):
+            rows_ps = psum.tile([P, BLOCKS, P], BF16, tag="to_scalar")
+            for tb in range(BLOCKS):
+                nc.tensor.transpose(rows_ps[:, tb, :], splits[k % 2][:, tb, :], ident_bf16[:])
+            gate_rows[k] = small.tile([P, BLOCKS, P], BF16, name="gate_rows%d" % k, tag="gate_rows")
+            nc.scalar.copy(out=gate_rows[k][:], in_=rows_ps[:])
+
+        def quantise_block(k, tb):
+            blk = k * BLOCKS + tb
+            nc.vector.quantize_mx(
+                out=g_codes[:, blk].rearrange("p g t -> p (g t)").bitcast(FP8X4),
+                scales=g_scales[:, blk].rearrange("p g t -> p (g t)"),
+                in_=gated[k, tb][:].rearrange("p g t j -> p (g t j)"),
+            )
+
+        def gate_group(k, i):
+            tb, g = i // PASSES, i % PASSES
+            if g == 0:
+                gated[k, tb] = gated_pool.tile([P, PASSES, P, PACK], BF16, name="gated%d%d" % (k, tb), tag="gated", align_bytes=64)
+            f_ps = psum.tile([P, PACK, P], F32, tag="to_vector")
+            for j in range(PACK):
+                ct = g * PACK + j
+                nc.tensor.matmul(
+                    f_ps[:, j, :],
+                    lhsT=kv_rows[:, k // 2, ct * P : (ct + 1) * P],
+                    rhs=gate_rows[k][:, tb, :],
+                    start=True,
+                    stop=True,
+                )
+            nc.vector.tensor_tensor(
+                out=gated[k, tb][:, g, :, :],
+                in0=u_tiles[k][:, g * PACK : (g + 1) * PACK, tb * P : (tb + 1) * P].rearrange("p j t -> p t j"),
+                in1=f_ps[:].rearrange("p j t -> p t j"),
+                op=ALU.mult,
+            )
+            if g == 0 and tb > 0:
+                quantise_block(k, tb - 1)
+
+        def stage2_tile(k, i):
+            tb, h = i // 2, i % 2
+            blk = k * BLOCKS + tb
+            cols = slice(h * HALF, (h + 1) * HALF)
+            y_ps = psum.tile([P, HALF], F32, tag="to_vector")
+            for g in range(PASSES):
+                nc.tensor.matmul_mx(
+                    out=y_ps[:],
+                    lhsT=g_codes[:, blk, g, :].bitcast(FP8X4),
+                    lhsT_scale=g_scales[:, blk, g, :],
+                    rhs=wo_codes[:, g, cols].bitcast(FP8X4),
+                    rhs_scale=wo_scales[:, g, cols],
+                    start=(g == 0),
+                    stop=(g == PASSES - 1),
+                )
+            y_sb = y_pool.tile([P, HALF], F32, tag="y")
+            nc.vector.tensor_tensor(out=y_sb[:], in0=y_ps[:], in1=bout_bc[:, cols], op=ALU.add)
+            first = (k % 2) * CHUNK + tb * P
+            nc.sync.dma_start(out=out[k // 2, first : first + P, cols], in_=y_sb[:])
+
+        pieces = {}
+        for s in range(CHUNKS + 2):
+            if 0 <= s - 1 < CHUNKS:
+                gate_scalars(s - 1)
+            for i in range(STEPS):
+                if s < CHUNKS:
+                    stage1_tile(s, i)
+                if s >= 2:
+                    stage2_tile(s - 2, i)
+                if s + 1 < CHUNKS:
+                    g, h = (i // 2) // 2, (i // 2) % 2
+                    cols = slice(h * (CHUNK // 2), (h + 1) * (CHUNK // 2))
+                    if i % 2 == 0:
+                        pieces[s] = regroup(x_raw[s + 1, g][:, :, cols], CHUNK // 2, CHUNK // 2 if s < 2 else 0)
+                    else:
+                        quantise(pieces[s], x_codes[:, s + 1, g, cols], x_scales[:, s + 1, g, cols])
+            if 0 <= s - 1 < CHUNKS:
+                gate_transposes(s - 1)
+            for i in range(STEPS + 1):
+                if s < CHUNKS and i < STEPS:
+                    norm_group(s, i)
+                if 0 <= s - 1 < CHUNKS and i >= 1:
+                    gate_group(s - 1, i - 1)
+                if s == 0 and i < STEPS:
+                    h, g = (i // 2) // 2, (i // 2) % 2
+                    cols = slice(h * HALF, (h + 1) * HALF)
+                    if i % 2 == 0:
+                        pieces[s] = regroup(wo_raw[g, h][:], HALF, HALF)
+                    else:
+                        quantise(pieces[s], wo_codes[:, g, cols], wo_scales[:, g, cols])
+            if 0 <= s - 1 < CHUNKS:
+                quantise_block(s - 1, BLOCKS - 1)

@@ -24,6 +24,7 @@ CHUNK = 512
 CHUNKS = IMAGES * PIXELS // CHUNK
 BLOCKS = CHUNK // P
 HALF = CHANNELS // 2
+QUARTER = CHUNK // 2
 STEPS = 8
 TERMS = 3
 
@@ -36,7 +37,6 @@ def tile_hydraattention_pb_kernel(tc, x, mask, W_q, b_q, kv_know, kv_mask, W_out
 
     with ExitStack() as ctx:
         keep = ctx.enter_context(tc.tile_pool(name="keep", bufs=1))
-        raw_pool = ctx.enter_context(tc.tile_pool(name="raw", bufs=12))
         grouped_pool = ctx.enter_context(tc.tile_pool(name="grouped", bufs=3))
         u_pool = ctx.enter_context(tc.tile_pool(name="u", bufs=3))
         small = ctx.enter_context(tc.tile_pool(name="small", bufs=2))
@@ -66,20 +66,27 @@ def tile_hydraattention_pb_kernel(tc, x, mask, W_q, b_q, kv_know, kv_mask, W_out
         splits = [split_a, split_b]
         minus_half = keep.tile([P, BLOCKS], F32)
 
-        def x_unit(k, g):
-            cols = slice((k % 2) * CHUNK, (k % 2 + 1) * CHUNK)
-            return x_rows[k // 2, g * K_PASS : (g + 1) * K_PASS, cols].rearrange("(p j) t -> p j t", j=PACK)
+        x_raw = {}
+        for b in range(IMAGES):
+            for g in range(PASSES):
+                x_raw[b, g] = keep.tile([P, PACK, PIXELS], BF16, name="x_raw%d%d" % (b, g))
+        wq_raw = [keep.tile([P, PACK, CHANNELS], BF16, name="wq_raw%d" % g) for g in range(PASSES)]
+        wo_raw = [keep.tile([P, PACK, CHANNELS], BF16, name="wo_raw%d" % g) for g in range(PASSES)]
 
-        def wq_unit(g, h):
-            return W_q[g * K_PASS : (g + 1) * K_PASS, h * HALF : (h + 1) * HALF].rearrange("(p j) n -> p j n", j=PACK)
+        def load_x(b, g, cols):
+            rows = x_rows[b, g * K_PASS : (g + 1) * K_PASS, cols]
+            nc.sync.dma_start(out=x_raw[b, g][:, :, cols], in_=rows.rearrange("(p j) t -> p j t", j=PACK))
 
-        def wo_unit(g, h):
-            return W_out[g * K_PASS : (g + 1) * K_PASS, h * HALF : (h + 1) * HALF].rearrange("(j p) n -> p j n", p=P)
+        def load_wq(g, cols):
+            rows = W_q[g * K_PASS : (g + 1) * K_PASS, cols]
+            nc.sync.dma_start(out=wq_raw[g][:, :, cols], in_=rows.rearrange("(p j) n -> p j n", j=PACK))
 
-        def load(source, label):
-            raw = raw_pool.tile([P, PACK, CHUNK], BF16, name=label, tag="raw")
-            nc.sync.dma_start(out=raw[:], in_=source)
-            return raw
+        def load_wo(g):
+            rows = W_out[g * K_PASS : (g + 1) * K_PASS, :]
+            nc.sync.dma_start(out=wo_raw[g][:], in_=rows.rearrange("(j p) n -> p j n", p=P))
+
+        first_half = slice(0, HALF)
+        second_half = slice(HALF, CHANNELS)
 
         nc.vector.memset(vectors[:], 0.0)
         nc.vector.memset(kv_rows[:], 0.0)
@@ -95,33 +102,26 @@ def tile_hydraattention_pb_kernel(tc, x, mask, W_q, b_q, kv_know, kv_mask, W_out
         nc.sync.dma_start(
             out=vectors[CHUNKS * BLOCKS : CHUNKS * BLOCKS + C_TILES, :], in_=b_q.rearrange("(r c) -> r c", c=P)
         )
-        x_raw = {}
-        wq_raw = {}
-        wo_raw = {}
-        x_raw[0, 0] = load(x_unit(0, 0), "x_raw00")
-        wq_raw[0, 0] = load(wq_unit(0, 0), "wq_raw00")
-        x_raw[0, 1] = load(x_unit(0, 1), "x_raw01")
-        wq_raw[1, 0] = load(wq_unit(1, 0), "wq_raw10")
-        wq_raw[0, 1] = load(wq_unit(0, 1), "wq_raw01")
-        wq_raw[1, 1] = load(wq_unit(1, 1), "wq_raw11")
         for g in range(PASSES):
-            x_raw[1, g] = load(x_unit(1, g), "x_raw1%d" % g)
-        for h in range(2):
-            for g in range(PASSES):
-                wo_raw[g, h] = load(wo_unit(g, h), "wo_raw%d%d" % (g, h))
-        for k in range(2, CHUNKS):
-            for g in range(PASSES):
-                x_raw[k, g] = load(x_unit(k, g), "x_raw%d%d" % (k, g))
-
-        nc.scalar.dma_start(
+            load_x(0, g, first_half)
+            load_wq(g, first_half)
+        for g in range(PASSES):
+            load_wq(g, second_half)
+        nc.sync.dma_start(
             out=kv_rows[0:TERMS].rearrange("r b c -> r (b c)"),
             in_=kv_know.rearrange("b o c -> (b o c)").partition_broadcast(TERMS),
         )
-        nc.scalar.dma_start(
+        nc.sync.dma_start(
             out=kv_rows[TERMS : 2 * TERMS].rearrange("r b c -> r (b c)"),
             in_=kv_mask.rearrange("b o c -> (b o c)").partition_broadcast(TERMS),
         )
-        nc.scalar.dma_start(out=bout_bc[:], in_=b_out.partition_broadcast(P))
+        for g in range(PASSES):
+            load_x(0, g, second_half)
+        for g in range(PASSES):
+            load_wo(g)
+        for g in range(PASSES):
+            load_x(1, g, slice(0, PIXELS))
+        nc.sync.dma_start(out=bout_bc[:], in_=b_out.partition_broadcast(P))
 
         def regroup(raw_cols, width, vector_cols):
             grouped = grouped_pool.tile([P, width, PACK], BF16, tag="grouped", align_bytes=64)
@@ -137,10 +137,20 @@ def tile_hydraattention_pb_kernel(tc, x, mask, W_q, b_q, kv_know, kv_mask, W_out
                 )
             return grouped
 
-        def quantise(grouped, codes, scales):
-            nc.vector.quantize_mx(
-                out=codes.bitcast(FP8X4), scales=scales, in_=grouped[:].rearrange("p w j -> p (w j)")
-            )
+        waiting = {"piece": None}
+
+        def quantise_waiting():
+            if waiting["piece"] is not None:
+                grouped, codes, scales = waiting["piece"]
+                nc.vector.quantize_mx(
+                    out=codes.bitcast(FP8X4), scales=scales, in_=grouped[:].rearrange("p w j -> p (w j)")
+                )
+                waiting["piece"] = None
+
+        def prepare(raw_cols, width, vector_cols, codes, scales):
+            grouped = regroup(raw_cols, width, vector_cols)
+            quantise_waiting()
+            waiting["piece"] = (grouped, codes, scales)
 
         vec_ps = psum.tile([P, P], BF16, tag="to_scalar")
         nc.tensor.transpose(vec_ps[:], vectors[:], ident_bf16[:])
@@ -154,21 +164,12 @@ def tile_hydraattention_pb_kernel(tc, x, mask, W_q, b_q, kv_know, kv_mask, W_out
         nc.vector.tensor_tensor(out=mix[:, :, 0], in0=blend[:], in1=inv[:], op=ALU.mult)
         nc.vector.scalar_tensor_tensor(out=mix[:, :, 1], in0=m_col, scalar=0.7, in1=m_col, op0=ALU.mult, op1=ALU.mult)
 
-        head = [
-            (x_raw[0, 0], x_codes[:, 0, 0, :], x_scales[:, 0, 0, :]),
-            (wq_raw[0, 0], wq_codes[:, 0, 0:HALF], wq_scales[:, 0, 0:HALF]),
-            (x_raw[0, 1], x_codes[:, 0, 1, :], x_scales[:, 0, 1, :]),
-            (wq_raw[1, 0], wq_codes[:, 1, 0:HALF], wq_scales[:, 1, 0:HALF]),
-            (wq_raw[0, 1], wq_codes[:, 0, HALF:CHANNELS], wq_scales[:, 0, HALF:CHANNELS]),
-            (wq_raw[1, 1], wq_codes[:, 1, HALF:CHANNELS], wq_scales[:, 1, HALF:CHANNELS]),
-        ]
-        waiting = None
-        for raw, codes, scales in head:
-            grouped = regroup(raw[:], CHUNK, CHUNK // 2)
-            if waiting is not None:
-                quantise(*waiting)
-            waiting = (grouped, codes, scales)
-        quantise(*waiting)
+        for g in range(PASSES):
+            prepare(x_raw[0, g][:, :, first_half], HALF, HALF // 2, x_codes[:, 0, g, :], x_scales[:, 0, g, :])
+            prepare(wq_raw[g][:, :, first_half], HALF, HALF // 2, wq_codes[:, g, first_half], wq_scales[:, g, first_half])
+        for g in range(PASSES):
+            prepare(wq_raw[g][:, :, second_half], HALF, HALF // 2, wq_codes[:, g, second_half], wq_scales[:, g, second_half])
+        quantise_waiting()
 
         u_tiles = {}
         sumsq_parts = {}
@@ -290,7 +291,6 @@ def tile_hydraattention_pb_kernel(tc, x, mask, W_q, b_q, kv_know, kv_mask, W_out
             first = (k % 2) * CHUNK + tb * P
             nc.sync.dma_start(out=out[k // 2, first : first + P, cols], in_=y_sb[:])
 
-        pieces = {}
         for s in range(CHUNKS + 2):
             if 0 <= s - 1 < CHUNKS:
                 gate_scalars(s - 1)
@@ -299,13 +299,15 @@ def tile_hydraattention_pb_kernel(tc, x, mask, W_q, b_q, kv_know, kv_mask, W_out
                     stage1_tile(s, i)
                 if s >= 2:
                     stage2_tile(s - 2, i)
-                if s + 1 < CHUNKS:
-                    g, h = (i // 2) // 2, (i // 2) % 2
-                    cols = slice(h * (CHUNK // 2), (h + 1) * (CHUNK // 2))
-                    if i % 2 == 0:
-                        pieces[s] = regroup(x_raw[s + 1, g][:, :, cols], CHUNK // 2, CHUNK // 2 if s < 2 else 0)
-                    else:
-                        quantise(pieces[s], x_codes[:, s + 1, g, cols], x_scales[:, s + 1, g, cols])
+                if s + 1 < CHUNKS and i % 2 == 0:
+                    k, g, h = s + 1, (i // 2) // 2, (i // 2) % 2
+                    cols = slice(h * QUARTER, (h + 1) * QUARTER)
+                    pixels = slice((k % 2) * CHUNK + h * QUARTER, (k % 2) * CHUNK + (h + 1) * QUARTER)
+                    prepare(
+                        x_raw[k // 2, g][:, :, pixels], QUARTER, QUARTER if s < 2 else 0,
+                        x_codes[:, k, g, cols], x_scales[:, k, g, cols],
+                    )
+            quantise_waiting()
             if 0 <= s - 1 < CHUNKS:
                 gate_transposes(s - 1)
             for i in range(STEPS + 1):
@@ -313,12 +315,10 @@ def tile_hydraattention_pb_kernel(tc, x, mask, W_q, b_q, kv_know, kv_mask, W_out
                     norm_group(s, i)
                 if 0 <= s - 1 < CHUNKS and i >= 1:
                     gate_group(s - 1, i - 1)
-                if s == 0 and i < STEPS:
-                    h, g = (i // 2) // 2, (i // 2) % 2
+                if s == 0 and i < STEPS and i % 2 == 0:
+                    g, h = (i // 2) // 2, (i // 2) % 2
                     cols = slice(h * HALF, (h + 1) * HALF)
-                    if i % 2 == 0:
-                        pieces[s] = regroup(wo_raw[g, h][:], HALF, HALF)
-                    else:
-                        quantise(pieces[s], wo_codes[:, g, cols], wo_scales[:, g, cols])
+                    prepare(wo_raw[g][:, :, cols], HALF, HALF, wo_codes[:, g, cols], wo_scales[:, g, cols])
+            quantise_waiting()
             if 0 <= s - 1 < CHUNKS:
                 quantise_block(s - 1, BLOCKS - 1)

@@ -64,33 +64,44 @@ def tile_hydraattention_pb_kernel(tc, x, mask, W_q, b_q, kv_know, kv_mask, W_out
         split_a = keep.tile([P, BLOCKS, P], BF16)
         split_b = keep.tile([P, BLOCKS, P], BF16)
         splits = [split_a, split_b]
-        minus_half = keep.tile([P, BLOCKS], F32)
+        warm = keep.tile([P, 2], F32)
 
-        x_raw = {}
-        for b in range(IMAGES):
-            for g in range(PASSES):
-                x_raw[b, g] = keep.tile([P, PACK, PIXELS], BF16, name="x_raw%d%d" % (b, g))
-        wq_raw = [keep.tile([P, PACK, CHANNELS], BF16, name="wq_raw%d" % g) for g in range(PASSES)]
+        first_half = slice(0, HALF)
+        second_half = slice(HALF, CHANNELS)
+        halves = [first_half, second_half]
+        x0_raw = {}
+        wq_raw = {}
+        for g in range(PASSES):
+            for h in range(2):
+                x0_raw[g, h] = keep.tile([P, PACK, CHUNK], BF16, name="x0_raw%d%d" % (g, h))
+                wq_raw[g, h] = keep.tile([P, PACK, HALF], BF16, name="wq_raw%d%d" % (g, h))
+        x1_raw = [keep.tile([P, PACK, PIXELS], BF16, name="x1_raw%d" % g) for g in range(PASSES)]
         wo_raw = [keep.tile([P, PACK, CHANNELS], BF16, name="wo_raw%d" % g) for g in range(PASSES)]
 
-        def load_x(b, g, cols):
-            rows = x_rows[b, g * K_PASS : (g + 1) * K_PASS, cols]
-            nc.sync.dma_start(out=x_raw[b, g][:, :, cols], in_=rows.rearrange("(p j) t -> p j t", j=PACK))
+        def load_x0(g, h):
+            rows = x_rows[0, g * K_PASS : (g + 1) * K_PASS, halves[h]]
+            nc.sync.dma_start(out=x0_raw[g, h][:], in_=rows.rearrange("(p j) t -> p j t", j=PACK))
 
-        def load_wq(g, cols):
-            rows = W_q[g * K_PASS : (g + 1) * K_PASS, cols]
-            nc.sync.dma_start(out=wq_raw[g][:, :, cols], in_=rows.rearrange("(p j) n -> p j n", j=PACK))
+        def load_wq(g, h):
+            rows = W_q[g * K_PASS : (g + 1) * K_PASS, halves[h]]
+            nc.sync.dma_start(out=wq_raw[g, h][:], in_=rows.rearrange("(p j) n -> p j n", j=PACK))
+
+        def load_x1(g):
+            rows = x_rows[1, g * K_PASS : (g + 1) * K_PASS, :]
+            nc.sync.dma_start(out=x1_raw[g][:], in_=rows.rearrange("(p j) t -> p j t", j=PACK))
 
         def load_wo(g):
             rows = W_out[g * K_PASS : (g + 1) * K_PASS, :]
             nc.sync.dma_start(out=wo_raw[g][:], in_=rows.rearrange("(j p) n -> p j n", p=P))
 
-        first_half = slice(0, HALF)
-        second_half = slice(HALF, CHANNELS)
+        def x_columns(k, g, first, width):
+            if k < 2:
+                return x0_raw[g, k][:, :, first : first + width]
+            return x1_raw[g][:, :, (k - 2) * CHUNK + first : (k - 2) * CHUNK + first + width]
 
         nc.vector.memset(vectors[:], 0.0)
         nc.vector.memset(kv_rows[:], 0.0)
-        nc.vector.memset(minus_half[:], -0.5)
+        nc.vector.memset(warm[:], 1.0)
         nc.vector.memset(split_a[:], 0.0)
         nc.vector.memset(split_b[:], 0.0)
         make_identity(nc, ident_bf16[:])
@@ -103,10 +114,10 @@ def tile_hydraattention_pb_kernel(tc, x, mask, W_q, b_q, kv_know, kv_mask, W_out
             out=vectors[CHUNKS * BLOCKS : CHUNKS * BLOCKS + C_TILES, :], in_=b_q.rearrange("(r c) -> r c", c=P)
         )
         for g in range(PASSES):
-            load_x(0, g, first_half)
-            load_wq(g, first_half)
+            load_x0(g, 0)
+            load_wq(g, 0)
         for g in range(PASSES):
-            load_wq(g, second_half)
+            load_wq(g, 1)
         nc.sync.dma_start(
             out=kv_rows[0:TERMS].rearrange("r b c -> r (b c)"),
             in_=kv_know.rearrange("b o c -> (b o c)").partition_broadcast(TERMS),
@@ -116,12 +127,14 @@ def tile_hydraattention_pb_kernel(tc, x, mask, W_q, b_q, kv_know, kv_mask, W_out
             in_=kv_mask.rearrange("b o c -> (b o c)").partition_broadcast(TERMS),
         )
         for g in range(PASSES):
-            load_x(0, g, second_half)
+            load_x0(g, 1)
         for g in range(PASSES):
             load_wo(g)
         for g in range(PASSES):
-            load_x(1, g, slice(0, PIXELS))
+            load_x1(g)
         nc.sync.dma_start(out=bout_bc[:], in_=b_out.partition_broadcast(P))
+
+        nc.scalar.activation(out=warm[:, 1:2], in_=warm[:, 0:1], func=ACT.Abs_reciprocal_sqrt)
 
         def regroup(raw_cols, width, vector_cols):
             grouped = grouped_pool.tile([P, width, PACK], BF16, tag="grouped", align_bytes=64)
@@ -165,10 +178,10 @@ def tile_hydraattention_pb_kernel(tc, x, mask, W_q, b_q, kv_know, kv_mask, W_out
         nc.vector.scalar_tensor_tensor(out=mix[:, :, 1], in0=m_col, scalar=0.7, in1=m_col, op0=ALU.mult, op1=ALU.mult)
 
         for g in range(PASSES):
-            prepare(x_raw[0, g][:, :, first_half], HALF, HALF // 2, x_codes[:, 0, g, :], x_scales[:, 0, g, :])
-            prepare(wq_raw[g][:, :, first_half], HALF, HALF // 2, wq_codes[:, g, first_half], wq_scales[:, g, first_half])
+            prepare(x_columns(0, g, 0, CHUNK), CHUNK, CHUNK // 2, x_codes[:, 0, g, :], x_scales[:, 0, g, :])
+            prepare(wq_raw[g, 0][:], HALF, HALF // 2, wq_codes[:, g, first_half], wq_scales[:, g, first_half])
         for g in range(PASSES):
-            prepare(wq_raw[g][:, :, second_half], HALF, HALF // 2, wq_codes[:, g, second_half], wq_scales[:, g, second_half])
+            prepare(wq_raw[g, 1][:], HALF, HALF // 2, wq_codes[:, g, second_half], wq_scales[:, g, second_half])
         quantise_waiting()
 
         u_tiles = {}
@@ -212,26 +225,31 @@ def tile_hydraattention_pb_kernel(tc, x, mask, W_q, b_q, kv_know, kv_mask, W_out
                 accum_out=sumsq_parts[k][:, tb, half : half + 1],
             )
 
-        def gate_scalars(k):
-            sumsq = small.tile([P, BLOCKS], F32, tag="sumsq")
+        def gate_scalars(k, engine):
             rnorm = small.tile([P, BLOCKS], F32, tag="rnorm")
             weights = small.tile([P, BLOCKS, 2], F32, tag="weights")
             rest1 = small.tile([P, BLOCKS, 2], F32, tag="rest1")
             rest2 = small.tile([P, BLOCKS, 2], F32, tag="rest2")
             split = splits[k % 2]
-            nc.gpsimd.tensor_tensor(out=sumsq[:], in0=sumsq_parts[k][:, :, 0], in1=sumsq_parts[k][:, :, 1], op=ALU.add)
-            nc.gpsimd.tensor_tensor(out=rnorm[:], in0=sumsq[:], in1=minus_half[:], op=ALU.pow)
-            nc.gpsimd.tensor_tensor(
+            for tb in range(BLOCKS):
+                nc.scalar.activation(
+                    out=rnorm[:, tb : tb + 1],
+                    in_=sumsq_parts[k][:, tb, 0:1],
+                    func=ACT.Abs_reciprocal_sqrt,
+                    bias=sumsq_parts[k][:, tb, 1:2],
+                    scale=1.0,
+                )
+            engine.tensor_tensor(
                 out=weights[:],
                 in0=mix[:, k * BLOCKS : (k + 1) * BLOCKS, :],
                 in1=rnorm[:].unsqueeze(2).to_broadcast([P, BLOCKS, 2]),
                 op=ALU.mult,
             )
-            nc.gpsimd.tensor_copy(out=split[:, :, 0 : 2 * TERMS : TERMS], in_=weights[:])
-            nc.gpsimd.tensor_tensor(out=rest1[:], in0=weights[:], in1=split[:, :, 0 : 2 * TERMS : TERMS], op=ALU.subtract)
-            nc.gpsimd.tensor_copy(out=split[:, :, 1 : 2 * TERMS : TERMS], in_=rest1[:])
-            nc.gpsimd.tensor_tensor(out=rest2[:], in0=rest1[:], in1=split[:, :, 1 : 2 * TERMS : TERMS], op=ALU.subtract)
-            nc.gpsimd.tensor_copy(out=split[:, :, 2 : 2 * TERMS : TERMS], in_=rest2[:])
+            engine.tensor_copy(out=split[:, :, 0 : 2 * TERMS : TERMS], in_=weights[:])
+            engine.tensor_tensor(out=rest1[:], in0=weights[:], in1=split[:, :, 0 : 2 * TERMS : TERMS], op=ALU.subtract)
+            engine.tensor_copy(out=split[:, :, 1 : 2 * TERMS : TERMS], in_=rest1[:])
+            engine.tensor_tensor(out=rest2[:], in0=rest1[:], in1=split[:, :, 1 : 2 * TERMS : TERMS], op=ALU.subtract)
+            engine.tensor_copy(out=split[:, :, 2 : 2 * TERMS : TERMS], in_=rest2[:])
 
         def gate_transposes(k):
             rows_ps = psum.tile([P, BLOCKS, P], BF16, tag="to_scalar")
@@ -293,7 +311,7 @@ def tile_hydraattention_pb_kernel(tc, x, mask, W_q, b_q, kv_know, kv_mask, W_out
 
         for s in range(CHUNKS + 2):
             if 0 <= s - 1 < CHUNKS:
-                gate_scalars(s - 1)
+                gate_scalars(s - 1, nc.vector if s == 1 else nc.gpsimd)
             for i in range(STEPS):
                 if s < CHUNKS:
                     stage1_tile(s, i)
@@ -302,9 +320,8 @@ def tile_hydraattention_pb_kernel(tc, x, mask, W_q, b_q, kv_know, kv_mask, W_out
                 if s + 1 < CHUNKS and i % 2 == 0:
                     k, g, h = s + 1, (i // 2) // 2, (i // 2) % 2
                     cols = slice(h * QUARTER, (h + 1) * QUARTER)
-                    pixels = slice((k % 2) * CHUNK + h * QUARTER, (k % 2) * CHUNK + (h + 1) * QUARTER)
                     prepare(
-                        x_raw[k // 2, g][:, :, pixels], QUARTER, QUARTER if s < 2 else 0,
+                        x_columns(k, g, h * QUARTER, QUARTER), QUARTER, QUARTER if s < 2 else 0,
                         x_codes[:, k, g, cols], x_scales[:, k, g, cols],
                     )
             quantise_waiting()

@@ -20,12 +20,14 @@ CHANNELS = 1024
 PIXELS = 1024
 PASSES = CHANNELS // K_PASS
 C_TILES = CHANNELS // P
-CHUNK = 512
-CHUNKS = IMAGES * PIXELS // CHUNK
-BLOCKS = CHUNK // P
+BLOCKS = IMAGES * PIXELS // P
+IMAGE_BLOCKS = PIXELS // P
+CHUNK_BLOCKS = [2] * (BLOCKS // 2)
+CHUNKS = len(CHUNK_BLOCKS)
+MAX_BLOCKS = max(CHUNK_BLOCKS)
+CHUNK_STARTS = [sum(CHUNK_BLOCKS[:k]) for k in range(CHUNKS)]
+STEPS = 4
 HALF = CHANNELS // 2
-QUARTER = CHUNK // 2
-STEPS = 8
 TERMS = 3
 
 FLOPS = 2 * 2 * IMAGES * PIXELS * CHANNELS * CHANNELS
@@ -37,7 +39,7 @@ def tile_hydraattention_pb_kernel(tc, x, mask, W_q, b_q, kv_know, kv_mask, W_out
 
     with ExitStack() as ctx:
         keep = ctx.enter_context(tc.tile_pool(name="keep", bufs=1))
-        grouped_pool = ctx.enter_context(tc.tile_pool(name="grouped", bufs=3))
+        grouped_pool = ctx.enter_context(tc.tile_pool(name="grouped", bufs=5))
         u_pool = ctx.enter_context(tc.tile_pool(name="u", bufs=3))
         small = ctx.enter_context(tc.tile_pool(name="small", bufs=2))
         junk_pool = ctx.enter_context(tc.tile_pool(name="junk", bufs=4))
@@ -50,19 +52,19 @@ def tile_hydraattention_pb_kernel(tc, x, mask, W_q, b_q, kv_know, kv_mask, W_out
         wq_scales = keep.tile([P, PASSES, CHANNELS], U8, align_bytes=64)
         wo_codes = keep.tile([P, PASSES, CHANNELS], U32, align_bytes=64)
         wo_scales = keep.tile([P, PASSES, CHANNELS], U8, align_bytes=64)
-        x_codes = keep.tile([P, CHUNKS, PASSES, CHUNK], U32, align_bytes=64)
-        x_scales = keep.tile([P, CHUNKS, PASSES, CHUNK], U8, align_bytes=64)
-        g_codes = keep.tile([P, CHUNKS * BLOCKS, PASSES, P], U32, align_bytes=64)
-        g_scales = keep.tile([P, CHUNKS * BLOCKS, PASSES, P], U8, align_bytes=64)
+        x_codes = keep.tile([P, BLOCKS * PASSES * P], U32, align_bytes=64)
+        x_scales = keep.tile([P, BLOCKS * PASSES * P], U8, align_bytes=64)
+        g_codes = keep.tile([P, BLOCKS, PASSES, P], U32, align_bytes=64)
+        g_scales = keep.tile([P, BLOCKS, PASSES, P], U8, align_bytes=64)
         ident_f32 = keep.tile([P, P], F32)
         ident_bf16 = keep.tile([P, P], BF16)
         vectors = keep.tile([P, P], BF16)
-        columns = keep.tile([P, CHUNKS * BLOCKS + C_TILES], F32)
-        mix = keep.tile([P, CHUNKS * BLOCKS, 2], F32)
+        columns = keep.tile([P, BLOCKS + C_TILES], F32)
+        mix = keep.tile([P, BLOCKS, 2], F32)
         kv_rows = keep.tile([P, IMAGES, CHANNELS], BF16)
         bout_bc = keep.tile([P, CHANNELS], BF16)
-        split_a = keep.tile([P, BLOCKS, P], BF16)
-        split_b = keep.tile([P, BLOCKS, P], BF16)
+        split_a = keep.tile([P, MAX_BLOCKS, P], BF16)
+        split_b = keep.tile([P, MAX_BLOCKS, P], BF16)
         splits = [split_a, split_b]
         warm = keep.tile([P, 2], F32)
 
@@ -73,7 +75,7 @@ def tile_hydraattention_pb_kernel(tc, x, mask, W_q, b_q, kv_know, kv_mask, W_out
         wq_raw = {}
         for g in range(PASSES):
             for h in range(2):
-                x0_raw[g, h] = keep.tile([P, PACK, CHUNK], BF16, name="x0_raw%d%d" % (g, h))
+                x0_raw[g, h] = keep.tile([P, PACK, HALF], BF16, name="x0_raw%d%d" % (g, h))
                 wq_raw[g, h] = keep.tile([P, PACK, HALF], BF16, name="wq_raw%d%d" % (g, h))
         x1_raw = [keep.tile([P, PACK, PIXELS], BF16, name="x1_raw%d" % g) for g in range(PASSES)]
         wo_raw = [keep.tile([P, PACK, CHANNELS], BF16, name="wo_raw%d" % g) for g in range(PASSES)]
@@ -94,10 +96,12 @@ def tile_hydraattention_pb_kernel(tc, x, mask, W_q, b_q, kv_know, kv_mask, W_out
             rows = W_out[g * K_PASS : (g + 1) * K_PASS, :]
             nc.sync.dma_start(out=wo_raw[g][:], in_=rows.rearrange("(j p) n -> p j n", p=P))
 
-        def x_columns(k, g, first, width):
-            if k < 2:
-                return x0_raw[g, k][:, :, first : first + width]
-            return x1_raw[g][:, :, (k - 2) * CHUNK + first : (k - 2) * CHUNK + first + width]
+        def x_columns(k, g):
+            image, first = divmod(CHUNK_STARTS[k] * P, PIXELS)
+            width = CHUNK_BLOCKS[k] * P
+            if image == 1:
+                return x1_raw[g][:, :, first : first + width]
+            return x0_raw[g, first // HALF][:, :, first % HALF : first % HALF + width]
 
         nc.vector.memset(vectors[:], 0.0)
         nc.vector.memset(kv_rows[:], 0.0)
@@ -108,16 +112,16 @@ def tile_hydraattention_pb_kernel(tc, x, mask, W_q, b_q, kv_know, kv_mask, W_out
         make_identity(nc, ident_f32[:])
 
         nc.sync.dma_start(
-            out=vectors[0 : CHUNKS * BLOCKS, :], in_=mask.rearrange("b o (r a) w -> (b o r) (a w)", a=4)
+            out=vectors[0 : BLOCKS, :], in_=mask.rearrange("b o (r a) w -> (b o r) (a w)", a=4)
         )
         nc.sync.dma_start(
-            out=vectors[CHUNKS * BLOCKS : CHUNKS * BLOCKS + C_TILES, :], in_=b_q.rearrange("(r c) -> r c", c=P)
+            out=vectors[BLOCKS : BLOCKS + C_TILES, :], in_=b_q.rearrange("(r c) -> r c", c=P)
         )
         for g in range(PASSES):
             load_x0(g, 0)
-            load_wq(g, 0)
-        for g in range(PASSES):
-            load_wq(g, 1)
+        for h in range(2):
+            for g in range(PASSES):
+                load_wq(g, h)
         nc.sync.dma_start(
             out=kv_rows[0:TERMS].rearrange("r b c -> r (b c)"),
             in_=kv_know.rearrange("b o c -> (b o c)").partition_broadcast(TERMS),
@@ -127,61 +131,94 @@ def tile_hydraattention_pb_kernel(tc, x, mask, W_q, b_q, kv_know, kv_mask, W_out
             in_=kv_mask.rearrange("b o c -> (b o c)").partition_broadcast(TERMS),
         )
         for g in range(PASSES):
-            load_x0(g, 1)
-        for g in range(PASSES):
             load_wo(g)
+        for g in range(PASSES):
+            load_x0(g, 1)
         for g in range(PASSES):
             load_x1(g)
         nc.sync.dma_start(out=bout_bc[:], in_=b_out.partition_broadcast(P))
 
         nc.scalar.activation(out=warm[:, 1:2], in_=warm[:, 0:1], func=ACT.Abs_reciprocal_sqrt)
 
-        def regroup(raw_cols, width, vector_cols):
-            grouped = grouped_pool.tile([P, width, PACK], BF16, tag="grouped", align_bytes=64)
-            if vector_cols > 0:
-                nc.vector.tensor_copy(
-                    out=grouped[:, 0:vector_cols, :].rearrange("p (c i) j -> p c j i", i=4),
-                    in_=raw_cols[:, :, 0:vector_cols].rearrange("p j (c i) -> p c j i", i=4),
-                )
-            if vector_cols < width:
-                nc.scalar.copy(
-                    out=grouped[:, vector_cols:width, :].rearrange("p (c i) j -> p c j i", i=4),
-                    in_=raw_cols[:, :, vector_cols:width].rearrange("p j (c i) -> p c j i", i=4),
-                )
-            return grouped
+        def regroup(engine_copy, grouped, raw_cols):
+            engine_copy(
+                out=grouped.rearrange("p (c i) j -> p c j i", i=4), in_=raw_cols.rearrange("p j (c i) -> p c j i", i=4)
+            )
+
+        def quantise(grouped, codes, scales):
+            nc.vector.quantize_mx(out=codes.bitcast(FP8X4), scales=scales, in_=grouped)
+
+        def new_grouped():
+            return grouped_pool.tile([P, HALF, PACK], BF16, name="grouped", tag="grouped", align_bytes=64)
 
         waiting = {"piece": None}
 
         def quantise_waiting():
             if waiting["piece"] is not None:
-                grouped, codes, scales = waiting["piece"]
-                nc.vector.quantize_mx(
-                    out=codes.bitcast(FP8X4), scales=scales, in_=grouped[:].rearrange("p w j -> p (w j)")
-                )
+                quantise(*waiting["piece"])
                 waiting["piece"] = None
 
-        def prepare(raw_cols, width, vector_cols, codes, scales):
-            grouped = regroup(raw_cols, width, vector_cols)
+        def queue_quantise(grouped, codes, scales):
             quantise_waiting()
-            waiting["piece"] = (grouped, codes, scales)
+            waiting["piece"] = (grouped.rearrange("p w j -> p (w j)"), codes, scales)
+
+        def prepare_wq(g, h):
+            grouped = new_grouped()
+            mid = HALF // 2
+            regroup(nc.vector.tensor_copy, grouped[:, 0:mid, :], wq_raw[g, h][:, :, 0:mid])
+            regroup(nc.scalar.copy, grouped[:, mid:HALF, :], wq_raw[g, h][:, :, mid:HALF])
+            queue_quantise(grouped[:], wq_codes[:, g, halves[h]], wq_scales[:, g, halves[h]])
+
+        def wo_piece(g, h, vector_cols):
+            grouped = new_grouped()
+            if vector_cols > 0:
+                regroup(nc.vector.tensor_copy, grouped[:, 0:vector_cols, :], wo_raw[g][:, :, h * HALF : h * HALF + vector_cols])
+            if vector_cols < HALF:
+                regroup(nc.scalar.copy, grouped[:, vector_cols:HALF, :], wo_raw[g][:, :, h * HALF + vector_cols : (h + 1) * HALF])
+            queue_quantise(grouped[:], wo_codes[:, g, halves[h]], wo_scales[:, g, halves[h]])
+
+        x_grouped = {}
+
+        def x_piece(k, g, engine_copy, first, width):
+            if k not in x_grouped:
+                x_grouped[k] = new_grouped()
+            regroup(
+                engine_copy,
+                x_grouped[k][:, g * CHUNK_BLOCKS[k] * P + first : g * CHUNK_BLOCKS[k] * P + first + width, :],
+                x_columns(k, g)[:, :, first : first + width],
+            )
+
+        def x_slice(k, g, passes=1):
+            width = CHUNK_BLOCKS[k] * P
+            first = CHUNK_STARTS[k] * PASSES * P + g * width
+            return slice(first, first + passes * width)
+
+        def queue_x(k):
+            cols = x_slice(k, 0, PASSES)
+            queue_quantise(x_grouped[k][:, 0 : CHUNK_BLOCKS[k] * PASSES * P, :], x_codes[:, cols], x_scales[:, cols])
+
+        for g in range(PASSES):
+            mid = CHUNK_BLOCKS[0] * P // 2
+            x_piece(0, g, nc.vector.tensor_copy, 0, mid)
+            x_piece(0, g, nc.scalar.copy, mid, mid)
+        queue_x(0)
+        prepare_wq(0, 0)
 
         vec_ps = psum.tile([P, P], BF16, tag="to_scalar")
         nc.tensor.transpose(vec_ps[:], vectors[:], ident_bf16[:])
-        nc.vector.tensor_copy(out=columns[:], in_=vec_ps[:, 0 : CHUNKS * BLOCKS + C_TILES])
-        m_col = columns[:, 0 : CHUNKS * BLOCKS]
-        bq_col = columns[:, CHUNKS * BLOCKS : CHUNKS * BLOCKS + C_TILES]
-        inv = keep.tile([P, CHUNKS * BLOCKS], F32)
-        blend = keep.tile([P, CHUNKS * BLOCKS], F32)
+        nc.vector.tensor_copy(out=columns[:], in_=vec_ps[:, 0 : BLOCKS + C_TILES])
+        m_col = columns[:, 0 : BLOCKS]
+        bq_col = columns[:, BLOCKS : BLOCKS + C_TILES]
+        inv = keep.tile([P, BLOCKS], F32)
+        blend = keep.tile([P, BLOCKS], F32)
         nc.vector.tensor_scalar(out=inv[:], in0=m_col, scalar1=-1.0, scalar2=1.0, op0=ALU.mult, op1=ALU.add)
         nc.vector.scalar_tensor_tensor(out=blend[:], in0=m_col, scalar=0.3, in1=inv[:], op0=ALU.mult, op1=ALU.add)
         nc.vector.tensor_tensor(out=mix[:, :, 0], in0=blend[:], in1=inv[:], op=ALU.mult)
         nc.vector.scalar_tensor_tensor(out=mix[:, :, 1], in0=m_col, scalar=0.7, in1=m_col, op0=ALU.mult, op1=ALU.mult)
 
+        prepare_wq(1, 0)
         for g in range(PASSES):
-            prepare(x_columns(0, g, 0, CHUNK), CHUNK, CHUNK // 2, x_codes[:, 0, g, :], x_scales[:, 0, g, :])
-            prepare(wq_raw[g, 0][:], HALF, HALF // 2, wq_codes[:, g, first_half], wq_scales[:, g, first_half])
-        for g in range(PASSES):
-            prepare(wq_raw[g, 1][:], HALF, HALF // 2, wq_codes[:, g, second_half], wq_scales[:, g, second_half])
+            prepare_wq(g, 1)
         quantise_waiting()
 
         u_tiles = {}
@@ -189,29 +226,34 @@ def tile_hydraattention_pb_kernel(tc, x, mask, W_q, b_q, kv_know, kv_mask, W_out
         gate_rows = {}
         gated = {}
 
-        def stage1_tile(k, ct):
-            if ct == 0:
-                u_tiles[k] = u_pool.tile([P, C_TILES, CHUNK], F32, name="u%d" % k, tag="u")
-            q_ps = psum.tile([P, CHUNK], F32, tag="to_scalar")
-            cols = slice(ct * P, (ct + 1) * P)
-            for g in range(PASSES):
-                nc.tensor.matmul_mx(
-                    out=q_ps[:],
-                    lhsT=wq_codes[:, g, cols].bitcast(FP8X4),
-                    lhsT_scale=wq_scales[:, g, cols],
-                    rhs=x_codes[:, k, g, :].bitcast(FP8X4),
-                    rhs_scale=x_scales[:, k, g, :],
-                    start=(g == 0),
-                    stop=(g == PASSES - 1),
+        def stage1_tile(k, i):
+            width = CHUNK_BLOCKS[k] * P
+            tiles = HALF // width
+            if i == 0:
+                u_tiles[k] = u_pool.tile([P, C_TILES, width], F32, name="u%d" % k, tag="u")
+            q_ps = psum.tile([P, tiles, width], F32, tag="to_scalar")
+            for e in range(tiles):
+                cols = slice((i * tiles + e) * P, (i * tiles + e + 1) * P)
+                for g in range(PASSES):
+                    nc.tensor.matmul_mx(
+                        out=q_ps[:, e, :],
+                        lhsT=wq_codes[:, g, cols].bitcast(FP8X4),
+                        lhsT_scale=wq_scales[:, g, cols],
+                        rhs=x_codes[:, x_slice(k, g)].bitcast(FP8X4),
+                        rhs_scale=x_scales[:, x_slice(k, g)],
+                        start=(g == 0),
+                        stop=(g == PASSES - 1),
+                    )
+            for e in range(tiles):
+                ct = i * tiles + e
+                nc.scalar.activation(
+                    out=u_tiles[k][:, ct, :], in_=q_ps[:, e, :], func=ACT.Identity, bias=bq_col[:, ct : ct + 1], scale=1.0
                 )
-            nc.scalar.activation(
-                out=u_tiles[k][:, ct, :], in_=q_ps[:], func=ACT.Identity, bias=bq_col[:, ct : ct + 1], scale=1.0
-            )
 
         def norm_group(k, i):
-            half, tb = i // BLOCKS, i % BLOCKS
+            half, tb = divmod(i, CHUNK_BLOCKS[k])
             if i == 0:
-                sumsq_parts[k] = small.tile([P, BLOCKS, 2], F32, name="parts%d" % k, tag="parts")
+                sumsq_parts[k] = small.tile([P, CHUNK_BLOCKS[k], 2], F32, name="parts%d" % k, tag="parts")
             ut_ps = psum.tile([P, PACK, P], F32, tag="to_scalar")
             for j in range(PACK):
                 nc.tensor.transpose(
@@ -226,12 +268,12 @@ def tile_hydraattention_pb_kernel(tc, x, mask, W_q, b_q, kv_know, kv_mask, W_out
             )
 
         def gate_scalars(k, engine):
-            rnorm = small.tile([P, BLOCKS], F32, tag="rnorm")
-            weights = small.tile([P, BLOCKS, 2], F32, tag="weights")
-            rest1 = small.tile([P, BLOCKS, 2], F32, tag="rest1")
-            rest2 = small.tile([P, BLOCKS, 2], F32, tag="rest2")
+            blocks = CHUNK_BLOCKS[k]
+            rnorm = small.tile([P, blocks], F32, tag="rnorm")
+            weights = small.tile([P, blocks, 2], F32, tag="weights")
+            rest = small.tile([P, blocks, 2], F32, tag="rest")
             split = splits[k % 2]
-            for tb in range(BLOCKS):
+            for tb in range(blocks):
                 nc.scalar.activation(
                     out=rnorm[:, tb : tb + 1],
                     in_=sumsq_parts[k][:, tb, 0:1],
@@ -239,27 +281,25 @@ def tile_hydraattention_pb_kernel(tc, x, mask, W_q, b_q, kv_know, kv_mask, W_out
                     bias=sumsq_parts[k][:, tb, 1:2],
                     scale=1.0,
                 )
-            engine.tensor_tensor(
-                out=weights[:],
-                in0=mix[:, k * BLOCKS : (k + 1) * BLOCKS, :],
-                in1=rnorm[:].unsqueeze(2).to_broadcast([P, BLOCKS, 2]),
-                op=ALU.mult,
-            )
-            engine.tensor_copy(out=split[:, :, 0 : 2 * TERMS : TERMS], in_=weights[:])
-            engine.tensor_tensor(out=rest1[:], in0=weights[:], in1=split[:, :, 0 : 2 * TERMS : TERMS], op=ALU.subtract)
-            engine.tensor_copy(out=split[:, :, 1 : 2 * TERMS : TERMS], in_=rest1[:])
-            engine.tensor_tensor(out=rest2[:], in0=rest1[:], in1=split[:, :, 1 : 2 * TERMS : TERMS], op=ALU.subtract)
-            engine.tensor_copy(out=split[:, :, 2 : 2 * TERMS : TERMS], in_=rest2[:])
+            terms = [split[:, 0:blocks, t : 2 * TERMS : TERMS] for t in range(TERMS)]
+            chunk_mix = mix[:, CHUNK_STARTS[k] : CHUNK_STARTS[k] + blocks, :]
+            rnorm_bc = rnorm[:].unsqueeze(2).to_broadcast([P, blocks, 2])
+            engine.tensor_tensor(out=terms[0], in0=chunk_mix, in1=rnorm_bc, op=ALU.mult)
+            engine.tensor_tensor(out=weights[:], in0=chunk_mix, in1=rnorm_bc, op=ALU.mult)
+            engine.tensor_tensor(out=terms[1], in0=weights[:], in1=terms[0], op=ALU.subtract)
+            engine.tensor_tensor(out=rest[:], in0=weights[:], in1=terms[0], op=ALU.subtract)
+            engine.tensor_tensor(out=terms[2], in0=rest[:], in1=terms[1], op=ALU.subtract)
 
         def gate_transposes(k):
-            rows_ps = psum.tile([P, BLOCKS, P], BF16, tag="to_scalar")
-            for tb in range(BLOCKS):
+            blocks = CHUNK_BLOCKS[k]
+            rows_ps = psum.tile([P, blocks, P], BF16, tag="to_scalar")
+            for tb in range(blocks):
                 nc.tensor.transpose(rows_ps[:, tb, :], splits[k % 2][:, tb, :], ident_bf16[:])
-            gate_rows[k] = small.tile([P, BLOCKS, P], BF16, name="gate_rows%d" % k, tag="gate_rows")
+            gate_rows[k] = small.tile([P, blocks, P], BF16, name="gate_rows%d" % k, tag="gate_rows")
             nc.scalar.copy(out=gate_rows[k][:], in_=rows_ps[:])
 
         def quantise_block(k, tb):
-            blk = k * BLOCKS + tb
+            blk = CHUNK_STARTS[k] + tb
             nc.vector.quantize_mx(
                 out=g_codes[:, blk].rearrange("p g t -> p (g t)").bitcast(FP8X4),
                 scales=g_scales[:, blk].rearrange("p g t -> p (g t)"),
@@ -275,7 +315,7 @@ def tile_hydraattention_pb_kernel(tc, x, mask, W_q, b_q, kv_know, kv_mask, W_out
                 ct = g * PACK + j
                 nc.tensor.matmul(
                     f_ps[:, j, :],
-                    lhsT=kv_rows[:, k // 2, ct * P : (ct + 1) * P],
+                    lhsT=kv_rows[:, CHUNK_STARTS[k] // IMAGE_BLOCKS, ct * P : (ct + 1) * P],
                     rhs=gate_rows[k][:, tb, :],
                     start=True,
                     stop=True,
@@ -291,7 +331,7 @@ def tile_hydraattention_pb_kernel(tc, x, mask, W_q, b_q, kv_know, kv_mask, W_out
 
         def stage2_tile(k, i):
             tb, h = i // 2, i % 2
-            blk = k * BLOCKS + tb
+            blk = CHUNK_STARTS[k] + tb
             cols = slice(h * HALF, (h + 1) * HALF)
             y_ps = psum.tile([P, HALF], F32, tag="to_vector")
             for g in range(PASSES):
@@ -306,36 +346,35 @@ def tile_hydraattention_pb_kernel(tc, x, mask, W_q, b_q, kv_know, kv_mask, W_out
                 )
             y_sb = y_pool.tile([P, HALF], F32, tag="y")
             nc.vector.tensor_tensor(out=y_sb[:], in0=y_ps[:], in1=bout_bc[:, cols], op=ALU.add)
-            first = (k % 2) * CHUNK + tb * P
-            nc.sync.dma_start(out=out[k // 2, first : first + P, cols], in_=y_sb[:])
+            image, first = divmod(blk * P, PIXELS)
+            nc.sync.dma_start(out=out[image, first : first + P, cols], in_=y_sb[:])
 
+        wo_halves = [[(0, 0), (1, 0)], [(0, 1), (1, 1)]]
         for s in range(CHUNKS + 2):
-            if 0 <= s - 1 < CHUNKS:
-                gate_scalars(s - 1, nc.vector if s == 1 else nc.gpsimd)
+            first, middle, last = s < CHUNKS, 0 <= s - 1 < CHUNKS, s >= 2
             for i in range(STEPS):
-                if s < CHUNKS:
+                if first:
                     stage1_tile(s, i)
-                if s >= 2:
+                if i == 0 and middle:
+                    gate_scalars(s - 1, nc.vector if s == 1 else nc.gpsimd)
+                if s + 1 < CHUNKS and i < 2:
+                    half = CHUNK_BLOCKS[s + 1] * P // 2
+                    x_piece(s + 1, 0, nc.vector.tensor_copy, i * half, half)
+                    x_piece(s + 1, 1, nc.vector.tensor_copy if s == 0 else nc.scalar.copy, i * half, half)
+            if s + 1 < CHUNKS:
+                queue_x(s + 1)
+            for g, h in wo_halves[s] if s < 2 else []:
+                wo_piece(g, h, HALF)
+            quantise_waiting()
+            if last:
+                for i in range(STEPS):
                     stage2_tile(s - 2, i)
-                if s + 1 < CHUNKS and i % 2 == 0:
-                    k, g, h = s + 1, (i // 2) // 2, (i // 2) % 2
-                    cols = slice(h * QUARTER, (h + 1) * QUARTER)
-                    prepare(
-                        x_columns(k, g, h * QUARTER, QUARTER), QUARTER, QUARTER if s < 2 else 0,
-                        x_codes[:, k, g, cols], x_scales[:, k, g, cols],
-                    )
-            quantise_waiting()
-            if 0 <= s - 1 < CHUNKS:
+            if middle:
                 gate_transposes(s - 1)
-            for i in range(STEPS + 1):
-                if s < CHUNKS and i < STEPS:
+            if first:
+                for i in range(STEPS):
                     norm_group(s, i)
-                if 0 <= s - 1 < CHUNKS and i >= 1:
-                    gate_group(s - 1, i - 1)
-                if s == 0 and i < STEPS and i % 2 == 0:
-                    g, h = (i // 2) // 2, (i // 2) % 2
-                    cols = slice(h * HALF, (h + 1) * HALF)
-                    prepare(wo_raw[g][:, :, cols], HALF, HALF, wo_codes[:, g, cols], wo_scales[:, g, cols])
-            quantise_waiting()
-            if 0 <= s - 1 < CHUNKS:
-                quantise_block(s - 1, BLOCKS - 1)
+            if middle:
+                for i in range(STEPS):
+                    gate_group(s - 1, i)
+                quantise_block(s - 1, CHUNK_BLOCKS[s - 1] - 1)

@@ -320,10 +320,11 @@ def tile_hydraattention_pb_kernel(tc, x, mask, W_q, b_q, kv_know, kv_mask, W_out
                     start=True,
                     stop=True,
                 )
+            u_block = u_tiles[k][:, g * PACK : (g + 1) * PACK, tb * P : (tb + 1) * P]
             nc.vector.tensor_tensor(
-                out=gated[k, tb][:, g, :, :],
-                in0=u_tiles[k][:, g * PACK : (g + 1) * PACK, tb * P : (tb + 1) * P].rearrange("p j t -> p t j"),
-                in1=f_ps[:].rearrange("p j t -> p t j"),
+                out=gated[k, tb][:, g, :, :].rearrange("p (c i) j -> p c j i", i=2),
+                in0=u_block.rearrange("p j (c i) -> p c j i", i=2),
+                in1=f_ps[:].rearrange("p j (c i) -> p c j i", i=2),
                 op=ALU.mult,
             )
             if g == 0 and tb > 0:

@@ -71,22 +71,22 @@ def tile_hydraattention_pb_kernel(tc, x, mask, W_q, b_q, kv_know, kv_mask, W_out
         first_half = slice(0, HALF)
         second_half = slice(HALF, CHANNELS)
         halves = [first_half, second_half]
+        x0_parts = [slice(0, 2 * P), slice(2 * P, 4 * P), slice(4 * P, PIXELS)]
         x0_raw = {}
-        wq_raw = {}
         for g in range(PASSES):
-            for h in range(2):
-                x0_raw[g, h] = keep.tile([P, PACK, HALF], BF16, name="x0_raw%d%d" % (g, h))
-                wq_raw[g, h] = keep.tile([P, PACK, HALF], BF16, name="wq_raw%d%d" % (g, h))
+            for h, part in enumerate(x0_parts):
+                x0_raw[g, h] = keep.tile([P, PACK, part.stop - part.start], BF16, name="x0_raw%d%d" % (g, h))
+        wq_raw = [keep.tile([P, PACK, CHANNELS], BF16, name="wq_raw%d" % g) for g in range(PASSES)]
         x1_raw = [keep.tile([P, PACK, PIXELS], BF16, name="x1_raw%d" % g) for g in range(PASSES)]
         wo_raw = [keep.tile([P, PACK, CHANNELS], BF16, name="wo_raw%d" % g) for g in range(PASSES)]
 
         def load_x0(g, h):
-            rows = x_rows[0, g * K_PASS : (g + 1) * K_PASS, halves[h]]
+            rows = x_rows[0, g * K_PASS : (g + 1) * K_PASS, x0_parts[h]]
             nc.sync.dma_start(out=x0_raw[g, h][:], in_=rows.rearrange("(p j) t -> p j t", j=PACK))
 
-        def load_wq(g, h):
-            rows = W_q[g * K_PASS : (g + 1) * K_PASS, halves[h]]
-            nc.sync.dma_start(out=wq_raw[g, h][:], in_=rows.rearrange("(p j) n -> p j n", j=PACK))
+        def load_wq(g):
+            rows = W_q[g * K_PASS : (g + 1) * K_PASS, :]
+            nc.sync.dma_start(out=wq_raw[g][:], in_=rows.rearrange("(p j) n -> p j n", j=PACK))
 
         def load_x1(g):
             rows = x_rows[1, g * K_PASS : (g + 1) * K_PASS, :]
@@ -101,7 +101,9 @@ def tile_hydraattention_pb_kernel(tc, x, mask, W_q, b_q, kv_know, kv_mask, W_out
             width = CHUNK_BLOCKS[k] * P
             if image == 1:
                 return x1_raw[g][:, :, first : first + width]
-            return x0_raw[g, first // HALF][:, :, first % HALF : first % HALF + width]
+            h = min(k, 2)
+            first -= x0_parts[h].start
+            return x0_raw[g, h][:, :, first : first + width]
 
         nc.vector.memset(vectors[:], 0.0)
         nc.vector.memset(kv_rows[:], 0.0)
@@ -119,9 +121,10 @@ def tile_hydraattention_pb_kernel(tc, x, mask, W_q, b_q, kv_know, kv_mask, W_out
         )
         for g in range(PASSES):
             load_x0(g, 0)
-        for h in range(2):
-            for g in range(PASSES):
-                load_wq(g, h)
+        for g in range(PASSES):
+            load_wq(g)
+        for g in range(PASSES):
+            load_x0(g, 1)
         nc.sync.dma_start(
             out=kv_rows[0:TERMS].rearrange("r b c -> r (b c)"),
             in_=kv_know.rearrange("b o c -> (b o c)").partition_broadcast(TERMS),
@@ -133,7 +136,7 @@ def tile_hydraattention_pb_kernel(tc, x, mask, W_q, b_q, kv_know, kv_mask, W_out
         for g in range(PASSES):
             load_wo(g)
         for g in range(PASSES):
-            load_x0(g, 1)
+            load_x0(g, 2)
         for g in range(PASSES):
             load_x1(g)
         nc.sync.dma_start(out=bout_bc[:], in_=b_out.partition_broadcast(P))
@@ -165,8 +168,9 @@ def tile_hydraattention_pb_kernel(tc, x, mask, W_q, b_q, kv_know, kv_mask, W_out
         def prepare_wq(g, h):
             grouped = new_grouped()
             mid = HALF // 2
-            regroup(nc.vector.tensor_copy, grouped[:, 0:mid, :], wq_raw[g, h][:, :, 0:mid])
-            regroup(nc.scalar.copy, grouped[:, mid:HALF, :], wq_raw[g, h][:, :, mid:HALF])
+            raw_cols = wq_raw[g][:, :, halves[h]]
+            regroup(nc.vector.tensor_copy, grouped[:, 0:mid, :], raw_cols[:, :, 0:mid])
+            regroup(nc.scalar.copy, grouped[:, mid:HALF, :], raw_cols[:, :, mid:HALF])
             queue_quantise(grouped[:], wq_codes[:, g, halves[h]], wq_scales[:, g, halves[h]])
 
         def wo_piece(g, h, vector_cols):
@@ -197,13 +201,6 @@ def tile_hydraattention_pb_kernel(tc, x, mask, W_q, b_q, kv_know, kv_mask, W_out
             cols = x_slice(k, 0, PASSES)
             queue_quantise(x_grouped[k][:, 0 : CHUNK_BLOCKS[k] * PASSES * P, :], x_codes[:, cols], x_scales[:, cols])
 
-        for g in range(PASSES):
-            mid = CHUNK_BLOCKS[0] * P // 2
-            x_piece(0, g, nc.vector.tensor_copy, 0, mid)
-            x_piece(0, g, nc.scalar.copy, mid, mid)
-        queue_x(0)
-        prepare_wq(0, 0)
-
         vec_ps = psum.tile([P, P], BF16, tag="to_scalar")
         nc.tensor.transpose(vec_ps[:], vectors[:], ident_bf16[:])
         nc.vector.tensor_copy(out=columns[:], in_=vec_ps[:, 0 : BLOCKS + C_TILES])
@@ -216,9 +213,14 @@ def tile_hydraattention_pb_kernel(tc, x, mask, W_q, b_q, kv_know, kv_mask, W_out
         nc.vector.tensor_tensor(out=mix[:, :, 0], in0=blend[:], in1=inv[:], op=ALU.mult)
         nc.vector.scalar_tensor_tensor(out=mix[:, :, 1], in0=m_col, scalar=0.7, in1=m_col, op0=ALU.mult, op1=ALU.mult)
 
-        prepare_wq(1, 0)
         for g in range(PASSES):
-            prepare_wq(g, 1)
+            mid = CHUNK_BLOCKS[0] * P // 2
+            x_piece(0, g, nc.vector.tensor_copy, 0, mid)
+            x_piece(0, g, nc.scalar.copy, mid, mid)
+        queue_x(0)
+        for g in range(PASSES):
+            for h in range(2):
+                prepare_wq(g, h)
         quantise_waiting()
 
         u_tiles = {}
@@ -350,7 +352,7 @@ def tile_hydraattention_pb_kernel(tc, x, mask, W_q, b_q, kv_know, kv_mask, W_out
             image, first = divmod(blk * P, PIXELS)
             nc.sync.dma_start(out=out[image, first : first + P, cols], in_=y_sb[:])
 
-        wo_halves = [[(0, 0), (1, 0)], [(0, 1), (1, 1)]]
+        wo_halves = [[(0, 0), (1, 0), (0, 1)], [(1, 1)]]
         for s in range(CHUNKS + 2):
             first, middle, last = s < CHUNKS, 0 <= s - 1 < CHUNKS, s >= 2
             for i in range(STEPS):

@@ -355,11 +355,11 @@ def tile_hydraattention_pb_kernel(tc, x, mask, W_q, b_q, kv_know, kv_mask, W_out
         wo_halves = [[(0, 0), (1, 0), (0, 1)], [(1, 1)]]
         for s in range(CHUNKS + 2):
             first, middle, last = s < CHUNKS, 0 <= s - 1 < CHUNKS, s >= 2
+            if middle:
+                gate_scalars(s - 1, nc.vector if s == 1 else nc.gpsimd)
             for i in range(STEPS):
                 if first:
                     stage1_tile(s, i)
-                if i == 0 and middle:
-                    gate_scalars(s - 1, nc.vector if s == 1 else nc.gpsimd)
                 if s + 1 < CHUNKS and i < 2:
                     half = CHUNK_BLOCKS[s + 1] * P // 2
                     x_piece(s + 1, 0, nc.vector.tensor_copy, i * half, half)
@@ -369,8 +369,9 @@ def tile_hydraattention_pb_kernel(tc, x, mask, W_q, b_q, kv_know, kv_mask, W_out
             for g, h in wo_halves[s] if s < 2 else []:
                 wo_piece(g, h, HALF)
             quantise_waiting()
+            early = {CHUNKS - 1: 2, CHUNKS: 1}.get(s, STEPS)
             if last:
-                for i in range(STEPS):
+                for i in range(early):
                     stage2_tile(s - 2, i)
             if middle:
                 gate_transposes(s - 1)
@@ -381,3 +382,6 @@ def tile_hydraattention_pb_kernel(tc, x, mask, W_q, b_q, kv_know, kv_mask, W_out
                 for i in range(STEPS):
                     gate_group(s - 1, i)
                 quantise_block(s - 1, CHUNK_BLOCKS[s - 1] - 1)
+            if last:
+                for i in range(early, STEPS):
+                    stage2_tile(s - 2, i)

@@ -28,6 +28,7 @@ MAX_BLOCKS = max(CHUNK_BLOCKS)
 CHUNK_STARTS = [sum(CHUNK_BLOCKS[:k]) for k in range(CHUNKS)]
 STEPS = 4
 HALF = CHANNELS // 2
+STAGGER = 64
 TERMS = 3
 
 FLOPS = 2 * 2 * IMAGES * PIXELS * CHANNELS * CHANNELS
@@ -48,14 +49,20 @@ def tile_hydraattention_pb_kernel(tc, x, mask, W_q, b_q, kv_know, kv_mask, W_out
         psum = ctx.enter_context(tc.psum_pool(name="psum", bufs=4))
         ctx.enter_context(tc.manual_schedule())
 
-        wq_codes = keep.tile([P, PASSES, CHANNELS], U32, align_bytes=64)
-        wq_scales = keep.tile([P, PASSES, CHANNELS], U8, align_bytes=64)
-        wo_codes = keep.tile([P, PASSES, CHANNELS], U32, align_bytes=64)
-        wo_scales = keep.tile([P, PASSES, CHANNELS], U8, align_bytes=64)
-        x_codes = keep.tile([P, BLOCKS * PASSES * P], U32, align_bytes=64)
-        x_scales = keep.tile([P, BLOCKS * PASSES * P], U8, align_bytes=64)
-        g_codes = keep.tile([P, BLOCKS, PASSES, P], U32, align_bytes=64)
-        g_scales = keep.tile([P, BLOCKS, PASSES, P], U8, align_bytes=64)
+        def operand(name, columns):
+            codes = keep.tile([P, columns + STAGGER // 4], U32, name=name + "_codes", align_bytes=64)
+            scales = keep.tile([P, columns + STAGGER], U8, name=name + "_scales", align_bytes=64)
+            return codes[:, 0:columns], scales[:, 0:columns]
+
+        def by_pass(plane):
+            return plane.rearrange("p (g n) -> p g n", g=PASSES)
+
+        wq_codes, wq_scales = (by_pass(plane) for plane in operand("wq", PASSES * CHANNELS))
+        x_codes, x_scales = operand("x", BLOCKS * PASSES * P)
+        wo_codes, wo_scales = (by_pass(plane) for plane in operand("wo", PASSES * CHANNELS))
+        g_codes, g_scales = (
+            plane.rearrange("p (b g t) -> p b g t", b=BLOCKS, g=PASSES) for plane in operand("g", BLOCKS * PASSES * P)
+        )
         ident_f32 = keep.tile([P, P], F32)
         ident_bf16 = keep.tile([P, P], BF16)
         vectors = keep.tile([P, P], BF16)

@@ -126,10 +126,10 @@ def tile_hydraattention_pb_kernel(tc, x, mask, W_q, b_q, kv_know, kv_mask, W_out
         nc.sync.dma_start(
             out=vectors[BLOCKS : BLOCKS + C_TILES, :], in_=b_q.rearrange("(r c) -> r c", c=P)
         )
+        load_wq(0)
         for g in range(PASSES):
             load_x0(g, 0)
-        for g in range(PASSES):
-            load_wq(g)
+        load_wq(1)
         for g in range(PASSES):
             load_x0(g, 1)
         nc.sync.dma_start(
@@ -220,14 +220,15 @@ def tile_hydraattention_pb_kernel(tc, x, mask, W_q, b_q, kv_know, kv_mask, W_out
         nc.vector.tensor_tensor(out=mix[:, :, 0], in0=blend[:], in1=inv[:], op=ALU.mult)
         nc.vector.scalar_tensor_tensor(out=mix[:, :, 1], in0=m_col, scalar=0.7, in1=m_col, op0=ALU.mult, op1=ALU.mult)
 
+        for h in range(2):
+            prepare_wq(0, h)
         for g in range(PASSES):
             mid = CHUNK_BLOCKS[0] * P // 2
             x_piece(0, g, nc.vector.tensor_copy, 0, mid)
             x_piece(0, g, nc.scalar.copy, mid, mid)
         queue_x(0)
-        for g in range(PASSES):
-            for h in range(2):
-                prepare_wq(g, h)
+        for h in range(2):
+            prepare_wq(1, h)
         quantise_waiting()
 
         u_tiles = {}
@@ -364,6 +365,8 @@ def tile_hydraattention_pb_kernel(tc, x, mask, W_q, b_q, kv_know, kv_mask, W_out
             first, middle, last = s < CHUNKS, 0 <= s - 1 < CHUNKS, s >= 2
             if middle:
                 gate_scalars(s - 1, nc.vector if s == 1 else nc.gpsimd)
+            if last and s + 1 >= CHUNKS:
+                quantise_block(s - 2, CHUNK_BLOCKS[s - 2] - 1)
             for i in range(STEPS):
                 if first:
                     stage1_tile(s, i)
@@ -371,15 +374,20 @@ def tile_hydraattention_pb_kernel(tc, x, mask, W_q, b_q, kv_know, kv_mask, W_out
                     half = CHUNK_BLOCKS[s + 1] * P // 2
                     x_piece(s + 1, 0, nc.vector.tensor_copy, i * half, half)
                     x_piece(s + 1, 1, nc.vector.tensor_copy if s == 0 else nc.scalar.copy, i * half, half)
+                    if i == 0 and last:
+                        quantise_block(s - 2, CHUNK_BLOCKS[s - 2] - 1)
             if s + 1 < CHUNKS:
                 queue_x(s + 1)
             for g, h in wo_halves[s] if s < 2 else []:
                 wo_piece(g, h, HALF)
-            quantise_waiting()
+            if s < 2:
+                quantise_waiting()
             early = {CHUNKS - 1: 2, CHUNKS: 1}.get(s, STEPS)
             if last:
                 for i in range(early):
                     stage2_tile(s - 2, i)
+                    if i == 1:
+                        quantise_waiting()
             if middle:
                 gate_transposes(s - 1)
             if first:
@@ -388,7 +396,6 @@ def tile_hydraattention_pb_kernel(tc, x, mask, W_q, b_q, kv_know, kv_mask, W_out
             if middle:
                 for i in range(STEPS):
                     gate_group(s - 1, i)
-                quantise_block(s - 1, CHUNK_BLOCKS[s - 1] - 1)
             if last:
                 for i in range(early, STEPS):
                     stage2_tile(s - 2, i)

@@ -294,11 +294,19 @@ def tile_hydraattention_pb_kernel(tc, x, mask, W_q, b_q, kv_know, kv_mask, W_out
             terms = [split[:, 0:blocks, t : 2 * TERMS : TERMS] for t in range(TERMS)]
             chunk_mix = mix[:, CHUNK_STARTS[k] : CHUNK_STARTS[k] + blocks, :]
             rnorm_bc = rnorm[:].unsqueeze(2).to_broadcast([P, blocks, 2])
-            engine.tensor_tensor(out=terms[0], in0=chunk_mix, in1=rnorm_bc, op=ALU.mult)
-            engine.tensor_tensor(out=weights[:], in0=chunk_mix, in1=rnorm_bc, op=ALU.mult)
-            engine.tensor_tensor(out=terms[1], in0=weights[:], in1=terms[0], op=ALU.subtract)
-            engine.tensor_tensor(out=rest[:], in0=weights[:], in1=terms[0], op=ALU.subtract)
-            engine.tensor_tensor(out=terms[2], in0=rest[:], in1=terms[1], op=ALU.subtract)
+
+            def term0():
+                engine.tensor_tensor(out=terms[0], in0=chunk_mix, in1=rnorm_bc, op=ALU.mult)
+                engine.tensor_tensor(out=weights[:], in0=chunk_mix, in1=rnorm_bc, op=ALU.mult)
+
+            def term1():
+                engine.tensor_tensor(out=terms[1], in0=weights[:], in1=terms[0], op=ALU.subtract)
+                engine.tensor_tensor(out=rest[:], in0=weights[:], in1=terms[0], op=ALU.subtract)
+
+            def term2():
+                engine.tensor_tensor(out=terms[2], in0=rest[:], in1=terms[1], op=ALU.subtract)
+
+            return [term0, term1, term2]
 
         def gate_transposes(k):
             blocks = CHUNK_BLOCKS[k]
@@ -363,19 +371,26 @@ def tile_hydraattention_pb_kernel(tc, x, mask, W_q, b_q, kv_know, kv_mask, W_out
         wo_halves = [[(0, 0), (1, 0), (0, 1)], [(1, 1)]]
         for s in range(CHUNKS + 2):
             first, middle, last = s < CHUNKS, 0 <= s - 1 < CHUNKS, s >= 2
-            if middle:
-                gate_scalars(s - 1, nc.vector if s == 1 else nc.gpsimd)
+            steps = gate_scalars(s - 1, (nc.gpsimd if s == CHUNKS else nc.vector)) if middle else []
+            if steps and s == 1:
+                steps.pop(0)()
             if last and s + 1 >= CHUNKS:
+                if steps:
+                    steps.pop(0)()
                 quantise_block(s - 2, CHUNK_BLOCKS[s - 2] - 1)
             for i in range(STEPS):
                 if first:
                     stage1_tile(s, i)
                 if s + 1 < CHUNKS and i < 2:
                     half = CHUNK_BLOCKS[s + 1] * P // 2
+                    if steps:
+                        steps.pop(0)()
                     x_piece(s + 1, 0, nc.vector.tensor_copy, i * half, half)
                     x_piece(s + 1, 1, nc.vector.tensor_copy if s == 0 else nc.scalar.copy, i * half, half)
                     if i == 0 and last:
                         quantise_block(s - 2, CHUNK_BLOCKS[s - 2] - 1)
+            while steps:
+                steps.pop(0)()
             if s + 1 < CHUNKS:
                 queue_x(s + 1)
             for g, h in wo_halves[s] if s < 2 else []:

@@ -49,20 +49,27 @@ def tile_hydraattention_pb_kernel(tc, x, mask, W_q, b_q, kv_know, kv_mask, W_out
         psum = ctx.enter_context(tc.psum_pool(name="psum", bufs=4))
         ctx.enter_context(tc.manual_schedule())
 
-        def operand(name, columns):
-            codes = keep.tile([P, columns + STAGGER // 4], U32, name=name + "_codes", align_bytes=64)
-            scales = keep.tile([P, columns + STAGGER], U8, name=name + "_scales", align_bytes=64)
-            return codes[:, 0:columns], scales[:, 0:columns]
+        def codes_tile(name, columns):
+            return keep.tile([P, columns + STAGGER // 4], U32, name=name + "_codes", align_bytes=64)[:, 0:columns]
+
+        def scales_tile(name, columns):
+            return keep.tile([P, columns + STAGGER], U8, name=name + "_scales", align_bytes=64)[:, 0:columns]
 
         def by_pass(plane):
             return plane.rearrange("p (g n) -> p g n", g=PASSES)
 
-        wq_codes, wq_scales = (by_pass(plane) for plane in operand("wq", PASSES * CHANNELS))
-        x_codes, x_scales = operand("x", BLOCKS * PASSES * P)
-        wo_codes, wo_scales = (by_pass(plane) for plane in operand("wo", PASSES * CHANNELS))
-        g_codes, g_scales = (
-            plane.rearrange("p (b g t) -> p b g t", b=BLOCKS, g=PASSES) for plane in operand("g", BLOCKS * PASSES * P)
-        )
+        def by_block(plane):
+            return plane.rearrange("p (b g t) -> p b g t", b=BLOCKS, g=PASSES)
+
+        w_columns, pixel_columns = PASSES * CHANNELS, BLOCKS * PASSES * P
+        wq_codes = by_pass(codes_tile("wq", w_columns))
+        x_codes = codes_tile("x", pixel_columns)
+        wq_scales = by_pass(scales_tile("wq", w_columns))
+        x_scales = scales_tile("x", pixel_columns)
+        wo_codes = by_pass(codes_tile("wo", w_columns))
+        g_codes = by_block(codes_tile("g", pixel_columns))
+        wo_scales = by_pass(scales_tile("wo", w_columns))
+        g_scales = by_block(scales_tile("g", pixel_columns))
         ident_f32 = keep.tile([P, P], F32)
         ident_bf16 = keep.tile([P, P], BF16)
         vectors = keep.tile([P, P], BF16)

@@ -404,7 +404,7 @@ def tile_hydraattention_pb_kernel(tc, x, mask, W_q, b_q, kv_know, kv_mask, W_out
                 wo_piece(g, h, HALF)
             if s < 2:
                 quantise_waiting()
-            early = {CHUNKS - 1: 2, CHUNKS: 1}.get(s, STEPS)
+            early = {CHUNKS - 1: 2, CHUNKS: 2}.get(s, STEPS)
             if last:
                 for i in range(early):
                     stage2_tile(s - 2, i)
@@ -412,11 +412,12 @@ def tile_hydraattention_pb_kernel(tc, x, mask, W_q, b_q, kv_know, kv_mask, W_out
                         quantise_waiting()
             if middle:
                 gate_transposes(s - 1)
-            if first:
-                for i in range(STEPS):
+            runs = 2 if s == CHUNKS - 1 else 1
+            for r in range(runs):
+                part = range(r * STEPS // runs, (r + 1) * STEPS // runs)
+                for i in part if first else []:
                     norm_group(s, i)
-            if middle:
-                for i in range(STEPS):
+                for i in part if middle else []:
                     gate_group(s - 1, i)
             if last:
                 for i in range(early, STEPS):

from contextlib import ExitStack

import concourse.mybir as mybir
from concourse.masks import make_identity

F32 = mybir.dt.float32
BF16 = mybir.dt.bfloat16
U32 = mybir.dt.uint32
U8 = mybir.dt.uint8
FP8X4 = mybir.dt.float8_e4m3fn_x4
ACT = mybir.ActivationFunctionType
ALU = mybir.AluOpType
AXIS = mybir.AxisListType

P = 128
PACK = 4
K_PASS = P * PACK
IMAGES = 2
CHANNELS = 1024
PIXELS = 1024
PASSES = CHANNELS // K_PASS
C_TILES = CHANNELS // P
BLOCKS = IMAGES * PIXELS // P
IMAGE_BLOCKS = PIXELS // P
CHUNK_BLOCKS = [2] * (BLOCKS // 2)
CHUNKS = len(CHUNK_BLOCKS)
MAX_BLOCKS = max(CHUNK_BLOCKS)
CHUNK_STARTS = [sum(CHUNK_BLOCKS[:k]) for k in range(CHUNKS)]
STEPS = 4
HALF = CHANNELS // 2
STAGGER = 64
TERMS = 3

FLOPS = 2 * 2 * IMAGES * PIXELS * CHANNELS * CHANNELS


def tile_hydraattention_pb_kernel(tc, x, mask, W_q, b_q, kv_know, kv_mask, W_out, b_out, out):
    nc = tc.nc
    x_rows = x.rearrange("b c h w -> b c (h w)")

    with ExitStack() as ctx:
        keep = ctx.enter_context(tc.tile_pool(name="keep", bufs=1))
        grouped_pool = ctx.enter_context(tc.tile_pool(name="grouped", bufs=5))
        u_pool = ctx.enter_context(tc.tile_pool(name="u", bufs=3))
        small = ctx.enter_context(tc.tile_pool(name="small", bufs=2))
        junk_pool = ctx.enter_context(tc.tile_pool(name="junk", bufs=4))
        gated_pool = ctx.enter_context(tc.tile_pool(name="gated", bufs=3))
        y_pool = ctx.enter_context(tc.tile_pool(name="y", bufs=8))
        psum = ctx.enter_context(tc.psum_pool(name="psum", bufs=4))
        ctx.enter_context(tc.manual_schedule())

        def codes_tile(name, columns):
            return keep.tile([P, columns + STAGGER // 4], U32, name=name + "_codes", align_bytes=64)[:, 0:columns]

        def scales_tile(name, columns):
            return keep.tile([P, columns + STAGGER], U8, name=name + "_scales", align_bytes=64)[:, 0:columns]

        def by_pass(plane):
            return plane.rearrange("p (g n) -> p g n", g=PASSES)

        def by_block(plane):
            return plane.rearrange("p (b g t) -> p b g t", b=BLOCKS, g=PASSES)

        w_columns, pixel_columns = PASSES * CHANNELS, BLOCKS * PASSES * P
        wq_codes = by_pass(codes_tile("wq", w_columns))
        x_codes = codes_tile("x", pixel_columns)
        wq_scales = by_pass(scales_tile("wq", w_columns))
        x_scales = scales_tile("x", pixel_columns)
        wo_codes = by_pass(codes_tile("wo", w_columns))
        g_codes = by_block(codes_tile("g", pixel_columns))
        wo_scales = by_pass(scales_tile("wo", w_columns))
        g_scales = by_block(scales_tile("g", pixel_columns))
        ident_f32 = keep.tile([P, P], F32)
        ident_bf16 = keep.tile([P, P], BF16)
        vectors = keep.tile([P, P], BF16)
        columns = keep.tile([P, BLOCKS + C_TILES], F32)
        mix = keep.tile([P, BLOCKS, 2], F32)
        kv_rows = keep.tile([P, IMAGES, CHANNELS], BF16)
        bout_bc = keep.tile([P, CHANNELS], BF16)
        split_a = keep.tile([P, MAX_BLOCKS, P], BF16)
        split_b = keep.tile([P, MAX_BLOCKS, P], BF16)
        splits = [split_a, split_b]
        warm = keep.tile([P, 2], F32)

        first_half = slice(0, HALF)
        second_half = slice(HALF, CHANNELS)
        halves = [first_half, second_half]
        x0_parts = [slice(0, 2 * P), slice(2 * P, 4 * P), slice(4 * P, PIXELS)]
        x0_raw = {}
        for g in range(PASSES):
            for h, part in enumerate(x0_parts):
                x0_raw[g, h] = keep.tile([P, PACK, part.stop - part.start], BF16, name="x0_raw%d%d" % (g, h))
        wq_raw = [keep.tile([P, PACK, CHANNELS], BF16, name="wq_raw%d" % g) for g in range(PASSES)]
        x1_raw = [keep.tile([P, PACK, PIXELS], BF16, name="x1_raw%d" % g) for g in range(PASSES)]
        wo_raw = [keep.tile([P, PACK, CHANNELS], BF16, name="wo_raw%d" % g) for g in range(PASSES)]

        def load_x0(g, h):
            rows = x_rows[0, g * K_PASS : (g + 1) * K_PASS, x0_parts[h]]
            nc.sync.dma_start(out=x0_raw[g, h][:], in_=rows.rearrange("(p j) t -> p j t", j=PACK))

        def load_wq(g):
            rows = W_q[g * K_PASS : (g + 1) * K_PASS, :]
            nc.sync.dma_start(out=wq_raw[g][:], in_=rows.rearrange("(p j) n -> p j n", j=PACK))

        def load_x1(g):
            rows = x_rows[1, g * K_PASS : (g + 1) * K_PASS, :]
            nc.sync.dma_start(out=x1_raw[g][:], in_=rows.rearrange("(p j) t -> p j t", j=PACK))

        def load_wo(g):
            rows = W_out[g * K_PASS : (g + 1) * K_PASS, :]
            nc.sync.dma_start(out=wo_raw[g][:], in_=rows.rearrange("(j p) n -> p j n", p=P))

        def x_columns(k, g):
            image, first = divmod(CHUNK_STARTS[k] * P, PIXELS)
            width = CHUNK_BLOCKS[k] * P
            if image == 1:
                return x1_raw[g][:, :, first : first + width]
            h = min(k, 2)
            first -= x0_parts[h].start
            return x0_raw[g, h][:, :, first : first + width]

        nc.vector.memset(vectors[:], 0.0)
        nc.vector.memset(kv_rows[:], 0.0)
        nc.vector.memset(warm[:], 1.0)
        nc.vector.memset(split_a[:], 0.0)
        nc.vector.memset(split_b[:], 0.0)
        make_identity(nc, ident_bf16[:])
        make_identity(nc, ident_f32[:])

        nc.sync.dma_start(
            out=vectors[0 : BLOCKS, :], in_=mask.rearrange("b o (r a) w -> (b o r) (a w)", a=4)
        )
        nc.sync.dma_start(
            out=vectors[BLOCKS : BLOCKS + C_TILES, :], in_=b_q.rearrange("(r c) -> r c", c=P)
        )
        load_wq(0)
        for g in range(PASSES):
            load_x0(g, 0)
        load_wq(1)
        for g in range(PASSES):
            load_x0(g, 1)
        nc.sync.dma_start(
            out=kv_rows[0:TERMS].rearrange("r b c -> r (b c)"),
            in_=kv_know.rearrange("b o c -> (b o c)").partition_broadcast(TERMS),
        )
        nc.sync.dma_start(
            out=kv_rows[TERMS : 2 * TERMS].rearrange("r b c -> r (b c)"),
            in_=kv_mask.rearrange("b o c -> (b o c)").partition_broadcast(TERMS),
        )
        for g in range(PASSES):
            load_wo(g)
        for g in range(PASSES):
            load_x0(g, 2)
        for g in range(PASSES):
            load_x1(g)
        nc.sync.dma_start(out=bout_bc[:], in_=b_out.partition_broadcast(P))

        nc.scalar.activation(out=warm[:, 1:2], in_=warm[:, 0:1], func=ACT.Abs_reciprocal_sqrt)

        def regroup(engine_copy, grouped, raw_cols):
            engine_copy(
                out=grouped.rearrange("p (c i) j -> p c j i", i=4), in_=raw_cols.rearrange("p j (c i) -> p c j i", i=4)
            )

        def quantise(grouped, codes, scales):
            nc.vector.quantize_mx(out=codes.bitcast(FP8X4), scales=scales, in_=grouped)

        def new_grouped():
            return grouped_pool.tile([P, HALF, PACK], BF16, name="grouped", tag="grouped", align_bytes=64)

        waiting = {"piece": None}

        def quantise_waiting():
            if waiting["piece"] is not None:
                quantise(*waiting["piece"])
                waiting["piece"] = None

        def queue_quantise(grouped, codes, scales):
            quantise_waiting()
            waiting["piece"] = (grouped.rearrange("p w j -> p (w j)"), codes, scales)

        def prepare_wq(g, h):
            grouped = new_grouped()
            mid = HALF // 2
            raw_cols = wq_raw[g][:, :, halves[h]]
            regroup(nc.vector.tensor_copy, grouped[:, 0:mid, :], raw_cols[:, :, 0:mid])
            regroup(nc.scalar.copy, grouped[:, mid:HALF, :], raw_cols[:, :, mid:HALF])
            queue_quantise(grouped[:], wq_codes[:, g, halves[h]], wq_scales[:, g, halves[h]])

        def wo_piece(g, h, vector_cols):
            grouped = new_grouped()
            if vector_cols > 0:
                regroup(nc.vector.tensor_copy, grouped[:, 0:vector_cols, :], wo_raw[g][:, :, h * HALF : h * HALF + vector_cols])
            if vector_cols < HALF:
                regroup(nc.scalar.copy, grouped[:, vector_cols:HALF, :], wo_raw[g][:, :, h * HALF + vector_cols : (h + 1) * HALF])
            queue_quantise(grouped[:], wo_codes[:, g, halves[h]], wo_scales[:, g, halves[h]])

        x_grouped = {}

        def x_piece(k, g, engine_copy, first, width):
            if k not in x_grouped:
                x_grouped[k] = new_grouped()
            regroup(
                engine_copy,
                x_grouped[k][:, g * CHUNK_BLOCKS[k] * P + first : g * CHUNK_BLOCKS[k] * P + first + width, :],
                x_columns(k, g)[:, :, first : first + width],
            )

        def x_slice(k, g, passes=1):
            width = CHUNK_BLOCKS[k] * P
            first = CHUNK_STARTS[k] * PASSES * P + g * width
            return slice(first, first + passes * width)

        def queue_x(k):
            cols = x_slice(k, 0, PASSES)
            queue_quantise(x_grouped[k][:, 0 : CHUNK_BLOCKS[k] * PASSES * P, :], x_codes[:, cols], x_scales[:, cols])

        vec_ps = psum.tile([P, P], BF16, tag="to_scalar")
        nc.tensor.transpose(vec_ps[:], vectors[:], ident_bf16[:])
        nc.vector.tensor_copy(out=columns[:], in_=vec_ps[:, 0 : BLOCKS + C_TILES])
        m_col = columns[:, 0 : BLOCKS]
        bq_col = columns[:, BLOCKS : BLOCKS + C_TILES]
        inv = keep.tile([P, BLOCKS], F32)
        blend = keep.tile([P, BLOCKS], F32)
        nc.vector.tensor_scalar(out=inv[:], in0=m_col, scalar1=-1.0, scalar2=1.0, op0=ALU.mult, op1=ALU.add)
        nc.vector.scalar_tensor_tensor(out=blend[:], in0=m_col, scalar=0.3, in1=inv[:], op0=ALU.mult, op1=ALU.add)
        nc.vector.tensor_tensor(out=mix[:, :, 0], in0=blend[:], in1=inv[:], op=ALU.mult)
        nc.vector.scalar_tensor_tensor(out=mix[:, :, 1], in0=m_col, scalar=0.7, in1=m_col, op0=ALU.mult, op1=ALU.mult)

        for h in range(2):
            prepare_wq(0, h)
        for g in range(PASSES):
            mid = CHUNK_BLOCKS[0] * P // 2
            x_piece(0, g, nc.vector.tensor_copy, 0, mid)
            x_piece(0, g, nc.scalar.copy, mid, mid)
        queue_x(0)
        for h in range(2):
            prepare_wq(1, h)
        quantise_waiting()

        u_tiles = {}
        sumsq_parts = {}
        gate_rows = {}
        gated = {}

        def stage1_tile(k, i):
            width = CHUNK_BLOCKS[k] * P
            tiles = HALF // width
            if i == 0:
                u_tiles[k] = u_pool.tile([P, C_TILES, width], F32, name="u%d" % k, tag="u")
            q_ps = psum.tile([P, tiles, width], F32, tag="to_scalar")
            for e in range(tiles):
                cols = slice((i * tiles + e) * P, (i * tiles + e + 1) * P)
                for g in range(PASSES):
                    nc.tensor.matmul_mx(
                        out=q_ps[:, e, :],
                        lhsT=wq_codes[:, g, cols].bitcast(FP8X4),
                        lhsT_scale=wq_scales[:, g, cols],
                        rhs=x_codes[:, x_slice(k, g)].bitcast(FP8X4),
                        rhs_scale=x_scales[:, x_slice(k, g)],
                        start=(g == 0),
                        stop=(g == PASSES - 1),
                    )
            for e in range(tiles):
                ct = i * tiles + e
                nc.scalar.activation(
                    out=u_tiles[k][:, ct, :], in_=q_ps[:, e, :], func=ACT.Identity, bias=bq_col[:, ct : ct + 1], scale=1.0
                )

        def norm_group(k, i):
            half, tb = divmod(i, CHUNK_BLOCKS[k])
            if i == 0:
                sumsq_parts[k] = small.tile([P, CHUNK_BLOCKS[k], 2], F32, name="parts%d" % k, tag="parts")
            ut_ps = psum.tile([P, PACK, P], F32, tag="to_scalar")
            for j in range(PACK):
                nc.tensor.transpose(
                    ut_ps[:, j, :], u_tiles[k][:, half * PACK + j, tb * P : (tb + 1) * P], ident_f32[:]
                )
            junk = junk_pool.tile([P, PACK * P], BF16, tag="junk")
            nc.scalar.activation(
                out=junk[:],
                in_=ut_ps[:].rearrange("p j c -> p (j c)"),
                func=ACT.Square,
                accum_out=sumsq_parts[k][:, tb, half : half + 1],
            )

        def gate_scalars(k, engine):
            blocks = CHUNK_BLOCKS[k]
            rnorm = small.tile([P, blocks], F32, tag="rnorm")
            weights = small.tile([P, blocks, 2], F32, tag="weights")
            rest = small.tile([P, blocks, 2], F32, tag="rest")
            split = splits[k % 2]
            for tb in range(blocks):
                nc.scalar.activation(
                    out=rnorm[:, tb : tb + 1],
                    in_=sumsq_parts[k][:, tb, 0:1],
                    func=ACT.Abs_reciprocal_sqrt,
                    bias=sumsq_parts[k][:, tb, 1:2],
                    scale=1.0,
                )
            terms = [split[:, 0:blocks, t : 2 * TERMS : TERMS] for t in range(TERMS)]
            chunk_mix = mix[:, CHUNK_STARTS[k] : CHUNK_STARTS[k] + blocks, :]
            rnorm_bc = rnorm[:].unsqueeze(2).to_broadcast([P, blocks, 2])

            def term0():
                engine.tensor_tensor(out=terms[0], in0=chunk_mix, in1=rnorm_bc, op=ALU.mult)
                engine.tensor_tensor(out=weights[:], in0=chunk_mix, in1=rnorm_bc, op=ALU.mult)

            def term1():
                engine.tensor_tensor(out=terms[1], in0=weights[:], in1=terms[0], op=ALU.subtract)
                engine.tensor_tensor(out=rest[:], in0=weights[:], in1=terms[0], op=ALU.subtract)

            def term2():
                engine.tensor_tensor(out=terms[2], in0=rest[:], in1=terms[1], op=ALU.subtract)

            return [term0, term1, term2]

        def gate_transposes(k):
            blocks = CHUNK_BLOCKS[k]
            rows_ps = psum.tile([P, blocks, P], BF16, tag="to_scalar")
            for tb in range(blocks):
                nc.tensor.transpose(rows_ps[:, tb, :], splits[k % 2][:, tb, :], ident_bf16[:])
            gate_rows[k] = small.tile([P, blocks, P], BF16, name="gate_rows%d" % k, tag="gate_rows")
            nc.scalar.copy(out=gate_rows[k][:], in_=rows_ps[:])

        def quantise_block(k, tb):
            blk = CHUNK_STARTS[k] + tb
            nc.vector.quantize_mx(
                out=g_codes[:, blk].rearrange("p g t -> p (g t)").bitcast(FP8X4),
                scales=g_scales[:, blk].rearrange("p g t -> p (g t)"),
                in_=gated[k, tb][:].rearrange("p g t j -> p (g t j)"),
            )

        def gate_group(k, i):
            tb, g = i // PASSES, i % PASSES
            if g == 0:
                gated[k, tb] = gated_pool.tile([P, PASSES, P, PACK], BF16, name="gated%d%d" % (k, tb), tag="gated", align_bytes=64)
            f_ps = psum.tile([P, PACK, P], F32, tag="to_vector")
            for j in range(PACK):
                ct = g * PACK + j
                nc.tensor.matmul(
                    f_ps[:, j, :],
                    lhsT=kv_rows[:, CHUNK_STARTS[k] // IMAGE_BLOCKS, ct * P : (ct + 1) * P],
                    rhs=gate_rows[k][:, tb, :],
                    start=True,
                    stop=True,
                )
            u_block = u_tiles[k][:, g * PACK : (g + 1) * PACK, tb * P : (tb + 1) * P]
            nc.vector.tensor_tensor(
                out=gated[k, tb][:, g, :, :].rearrange("p (c i) j -> p c j i", i=2),
                in0=u_block.rearrange("p j (c i) -> p c j i", i=2),
                in1=f_ps[:].rearrange("p j (c i) -> p c j i", i=2),
                op=ALU.mult,
            )
            if g == 0 and tb > 0:
                quantise_block(k, tb - 1)

        def stage2_tile(k, i):
            tb, h = i // 2, i % 2
            blk = CHUNK_STARTS[k] + tb
            cols = slice(h * HALF, (h + 1) * HALF)
            y_ps = psum.tile([P, HALF], F32, tag="to_vector")
            for g in range(PASSES):
                nc.tensor.matmul_mx(
                    out=y_ps[:],
                    lhsT=g_codes[:, blk, g, :].bitcast(FP8X4),
                    lhsT_scale=g_scales[:, blk, g, :],
                    rhs=wo_codes[:, g, cols].bitcast(FP8X4),
                    rhs_scale=wo_scales[:, g, cols],
                    start=(g == 0),
                    stop=(g == PASSES - 1),
                )
            y_sb = y_pool.tile([P, HALF], F32, tag="y")
            nc.vector.tensor_tensor(out=y_sb[:], in0=y_ps[:], in1=bout_bc[:, cols], op=ALU.add)
            image, first = divmod(blk * P, PIXELS)
            nc.sync.dma_start(out=out[image, first : first + P, cols], in_=y_sb[:])

        wo_halves = [[(0, 0), (1, 0), (0, 1)], [(1, 1)]]
        for s in range(CHUNKS + 2):
            first, middle, last = s < CHUNKS, 0 <= s - 1 < CHUNKS, s >= 2
            steps = gate_scalars(s - 1, (nc.gpsimd if s == CHUNKS else nc.vector)) if middle else []
            if steps and s == 1:
                steps.pop(0)()
            if last and s + 1 >= CHUNKS:
                if steps:
                    steps.pop(0)()
                quantise_block(s - 2, CHUNK_BLOCKS[s - 2] - 1)
            for i in range(STEPS):
                if first:
                    stage1_tile(s, i)
                if s + 1 < CHUNKS and i < 2:
                    half = CHUNK_BLOCKS[s + 1] * P // 2
                    if steps:
                        steps.pop(0)()
                    x_piece(s + 1, 0, nc.vector.tensor_copy, i * half, half)
                    x_piece(s + 1, 1, nc.vector.tensor_copy if s == 0 else nc.scalar.copy, i * half, half)
                    if i == 0 and last:
                        quantise_block(s - 2, CHUNK_BLOCKS[s - 2] - 1)
            while steps:
                steps.pop(0)()
            if s + 1 < CHUNKS:
                queue_x(s + 1)
            for g, h in wo_halves[s] if s < 2 else []:
                wo_piece(g, h, HALF)
            if s < 2:
                quantise_waiting()
            early = {CHUNKS - 1: 2, CHUNKS: 2}.get(s, STEPS)
            if last:
                for i in range(early):
                    stage2_tile(s - 2, i)
                    if i == 1:
                        quantise_waiting()
            if middle:
                gate_transposes(s - 1)
            runs = 2 if s == CHUNKS - 1 else 1
            for r in range(runs):
                part = range(r * STEPS // runs, (r + 1) * STEPS // runs)
                for i in part if first else []:
                    norm_group(s, i)
                for i in part if middle else []:
                    gate_group(s - 1, i)
            if last:
                for i in range(early, STEPS):
                    stage2_tile(s - 2, i)
